import numpy as np
import ml_dtypes


def mxq(x, axis, fmt="e4m3"):
    dtype, down = {"e4m3": (ml_dtypes.float8_e4m3fn, 7), "e5m2": (ml_dtypes.float8_e5m2, 14)}[fmt]
    v = np.moveaxis(np.asarray(x, np.float32).astype(ml_dtypes.bfloat16).astype(np.float64), axis, -1)
    blocks = v.reshape(v.shape[:-1] + (-1, 32))
    amax = np.abs(blocks).max(-1, keepdims=True)
    byte = np.maximum(np.where(amax > 0, np.frexp(amax)[1] - 1 + 127, 0) - down, 1)
    scale = np.exp2(byte - 127.0)
    codes = (blocks / scale).astype(np.float32).astype(dtype).astype(np.float64)
    return np.moveaxis((codes * scale).reshape(v.shape), -1, axis)


WIDE = False


def mx_kscale(k):
    if not WIDE:
        return np.ones(k)
    levels = np.array([10, -10, 5, -5, 0])
    a = np.random.permutation(np.resize(levels, k // 512 * 4)).reshape(k // 512, 4)
    idx = np.arange(k)
    return np.exp2(a[idx // 512, idx % 128 // 32])


BF16 = ml_dtypes.bfloat16


def bf(x):
    return np.asarray(x, np.float32).astype(BF16)


def f64(x):
    return np.asarray(x).astype(np.float64)


B, S, T, DIM, H = 1, 512, 512, 2048, 16
D = DIM // H


def split_heads(t):
    return t.reshape(B, S, H, D).transpose(0, 2, 1, 3)


def setup_inputs():
    s = mx_kscale(DIM)
    return {
        "q": bf(np.random.standard_normal((B, H, S, D)) * 1.4),
        "k_cache": bf(np.random.standard_normal((B, H, T, D)) * 1.4),
        "k_new": bf(np.random.standard_normal((B, H, S, D)) * 1.4),
        "x": bf(np.random.standard_normal((B, S, DIM)) * s),
        "Wv": bf(np.random.standard_normal((DIM, DIM)) / np.sqrt(DIM) / s[None, :]),
        "bv": bf(np.random.standard_normal(DIM) * 0.2),
        "v_cache": bf(np.random.standard_normal((B, H, T, D))),
    }


def reference(q, k_cache, k_new, x, Wv, bv, v_cache):
    v_new = split_heads((mxq(f64(x), 2, "e4m3") @ mxq(f64(Wv), 1, "e4m3").T) + f64(bv))
    v = np.concatenate([f64(v_cache), v_new], axis=2)
    qf = f64(q)
    s = np.concatenate([qf @ f64(k_cache).transpose(0, 1, 3, 2), qf @ f64(k_new).transpose(0, 1, 3, 2)], axis=3) * (1.0 / np.sqrt(D))
    mask = np.arange(T + S)[None, :] <= np.arange(S)[:, None] + T
    s = np.where(mask[None, None], s, -np.inf)
    e = np.exp(s - s.max(-1, keepdims=True))
    ctx = (mxq(e, 3, "e4m3") @ mxq(v, 2, "e4m3")) / e.sum(-1, keepdims=True)
    return ctx.transpose(0, 2, 1, 3).reshape(B, S, DIM), v_new

@@ -1,0 +1,458 @@
+from contextlib import ExitStack
+
+import concourse.mybir as mybir
+from concourse.masks import make_identity
+
+BF16 = mybir.dt.bfloat16
+F32 = mybir.dt.float32
+U32 = mybir.dt.uint32
+U8 = mybir.dt.uint8
+FP8X4 = mybir.dt.float8_e4m3fn_x4
+ALU = mybir.AluOpType
+ACT = mybir.ActivationFunctionType
+AXIS_X = mybir.AxisListType.X
+
+P = 128
+PACK = 4
+K_PASS = P * PACK
+HEADS = 16
+HEAD_DIM = 128
+NEW = 512
+CACHE = 512
+KEYS = CACHE + NEW
+DIM = HEADS * HEAD_DIM
+Q_TILES = NEW // P
+PROJ_PASSES = DIM // K_PASS
+CHUNK_HEADS = 4
+CHUNKS = HEADS // CHUNK_HEADS
+CHUNK_DIM = CHUNK_HEADS * HEAD_DIM
+SCORE_SCALE = 1.0 / (HEAD_DIM**0.5)
+MASKED = -1.0e30
+
+FLOPS = 2 * NEW * DIM * DIM + 2 * (2 * HEADS * NEW * KEYS * HEAD_DIM)
+
+
+UNITS = HEADS * Q_TILES
+UNITS_PER_CHUNK = CHUNK_HEADS * Q_TILES
+EXP_LAG = 1
+TURN_LAG = 2
+QUANTISE_LAG = 3
+GROUP_V_LAG = 6
+QUANTISE_V_LAG = 7
+PV_LAG = 8
+CTX_LAG = 9
+RELOAD_LAG = UNITS_PER_CHUNK - Q_TILES + GROUP_V_LAG + 1
+ROUNDS = UNITS - Q_TILES + CTX_LAG + 1
+
+
+def tile_attentionlayer_pa_kernel(tc, q, k_cache, k_new, x, Wv, bv, v_cache, out_0, out_1):
+    nc = tc.nc
+
+    q_rows = q.rearrange("b h s d -> (b h s) d")
+    k_cache_rows = k_cache.rearrange("b h s d -> (b h s) d")
+    k_new_rows = k_new.rearrange("b h s d -> (b h s) d")
+    v_cache_rows = v_cache.rearrange("b h s d -> (b h s) d")
+    x_rows = x.rearrange("b s k -> (b s) k")
+    ctx_out = out_0.rearrange("b s f -> (b s) f")
+    v_new_out = out_1.rearrange("b h s d -> (b h) s d").rearrange("h (u p e) d -> u e p h d", u=2, e=2)
+
+    with ExitStack() as stack:
+        stack.enter_context(tc.manual_schedule())
+        const = stack.enter_context(tc.tile_pool(name="const", bufs=1))
+        rows_pool = stack.enter_context(tc.tile_pool(name="rows", bufs=3))
+        qkv_pool = stack.enter_context(tc.tile_pool(name="qkv", bufs=2))
+        w_mx_pool = stack.enter_context(tc.tile_pool(name="w_mx", bufs=2))
+        v_new_pool = stack.enter_context(tc.tile_pool(name="v_new", bufs=2))
+        grouped_pool = stack.enter_context(tc.tile_pool(name="grouped", bufs=3))
+        head_pool = stack.enter_context(tc.tile_pool(name="head", bufs=2))
+        unit_pool = stack.enter_context(tc.tile_pool(name="unit", bufs=4))
+        e_mx_pool = stack.enter_context(tc.tile_pool(name="e_mx", bufs=2 * Q_TILES))
+        score_psum = stack.enter_context(tc.psum_pool(name="score_psum", bufs=2))
+        turned_psum = stack.enter_context(tc.psum_pool(name="turned_psum", bufs=2))
+        mx_psum = stack.enter_context(tc.psum_pool(name="mx_psum", bufs=2))
+
+        def load_weights(c):
+            w_sb = rows_pool.tile([P, PACK, DIM], BF16, tag="rows")
+            for a in range(CHUNK_DIM // P):
+                first = c * CHUNK_DIM + a * P
+                nc.sync.dma_start(out=w_sb[:, a, :], in_=Wv[first : first + P, :])
+            return w_sb
+
+        def load_heads(c):
+            first = c * CHUNK_HEADS * NEW
+            rows = slice(first, first + CHUNK_HEADS * NEW)
+            q_sb = qkv_pool.tile([P, CHUNK_HEADS * Q_TILES, HEAD_DIM], BF16)
+            kc_sb = qkv_pool.tile([P, CHUNK_HEADS * Q_TILES, HEAD_DIM], BF16)
+            kn_sb = qkv_pool.tile([P, CHUNK_HEADS * Q_TILES, HEAD_DIM], BF16)
+            nc.sync.dma_start(out=q_sb[:], in_=q_rows[rows, :].rearrange("(j p) d -> p j d", p=P))
+            nc.sync.dma_start(out=kc_sb[:], in_=k_cache_rows[rows, :].rearrange("(j p) d -> p j d", p=P))
+            nc.sync.dma_start(out=kn_sb[:], in_=k_new_rows[rows, :].rearrange("(j p) d -> p j d", p=P))
+            return q_sb, kc_sb, kn_sb
+
+        def load_cached_values(c):
+            first = c * CHUNK_HEADS * CACHE
+            rows = slice(first, first + CHUNK_HEADS * CACHE)
+            vc_sb = qkv_pool.tile([P, CHUNK_HEADS, PACK, HEAD_DIM], BF16)
+            nc.sync.dma_start(
+                out=vc_sb[:].rearrange("p h (u e) d -> p (h u) (e d)", e=2),
+                in_=v_cache_rows[rows, :].rearrange("(hu p e) d -> p hu (e d)", p=P, e=2),
+            )
+            return vc_sb
+
+        x_sb = rows_pool.tile([P, PACK, DIM], BF16, tag="rows")
+        for u in range(2):
+            nc.sync.dma_start(
+                out=x_sb[:, 2 * u : 2 * u + 2, :].rearrange("p e k -> p (e k)"),
+                in_=x_rows[256 * u : 256 * u + 256, :].rearrange("(p e) k -> p (e k)", e=2),
+            )
+        weights_sb = {0: load_weights(0)}
+        heads_sb = {0: load_heads(0)}
+        bias_bf = const.tile([P, DIM], BF16)
+        nc.sync.dma_start(out=bias_bf[:], in_=bv.partition_broadcast(P))
+        weights_sb[1] = load_weights(1)
+        cached_sb = {0: load_cached_values(0)}
+        heads_sb[1] = load_heads(1)
+        cached_sb[1] = load_cached_values(1)
+
+        warm = const.tile([P, 1], F32)
+        nc.vector.memset(warm[:], 0.0)
+        nc.scalar.activation(out=warm[:], in_=warm[:], func=ACT.Exp)
+        ident_f32 = const.tile([P, P], F32)
+        make_identity(nc, ident_f32[:])
+        ident_bf = const.tile([P, P], BF16)
+        make_identity(nc, ident_bf[:])
+        mask_f32 = const.tile([P, P], F32)
+        nc.gpsimd.memset(mask_f32[:], 0.0)
+        nc.gpsimd.affine_select(
+            out=mask_f32[:],
+            in_=mask_f32[:],
+            pattern=[[-1, P]],
+            compare_op=ALU.is_ge,
+            fill=MASKED,
+            base=0,
+            channel_multiplier=1,
+        )
+        mask_bf = const.tile([P, P], BF16)
+        nc.vector.tensor_copy(out=mask_bf[:], in_=mask_f32[:])
+        e_rows = {}
+        for i in range(Q_TILES):
+            for parity in range(2):
+                e_rows[i, parity] = const.tile([P, KEYS], BF16, name="e_rows_%d_%d" % (i, parity))
+                seen = CACHE + (i + 1) * P
+                if seen < KEYS:
+                    nc.vector.memset(e_rows[i, parity][:, seen:KEYS], 0.0)
+
+        def turn_rows(rows_sb, half, g, copy):
+            turned = turned_psum.tile([P, 512], F32, tag="turned")
+            for j in range(2):
+                words = rows_sb[:, 2 * half + j, :].bitcast(F32)
+                for u in range(2):
+                    first = (K_PASS // 2) * g + P * u
+                    nc.tensor.transpose(
+                        turned[:, (2 * j + u) * P : (2 * j + u + 1) * P], words[:, first : first + P], ident_f32[:]
+                    )
+            grouped = grouped_pool.tile([P, 2 * P * PACK], BF16, tag="grouped", align_bytes=64)
+            copy(
+                out=grouped[:].bitcast(F32).rearrange("p (j m u) -> p j m u", j=2, u=2),
+                in_=turned[:].rearrange("p (j u m) -> p j m u", j=2, u=2),
+            )
+            return grouped
+
+        def quantise_rows(grouped, half, g, codes, scales):
+            columns = slice(2 * P * half, 2 * P * (half + 1))
+            nc.vector.quantize_mx(out=codes[:, g, columns].bitcast(FP8X4), scales=scales[:, g, columns], in_=grouped[:])
+
+        def new_weights_mx():
+            w_codes = w_mx_pool.tile([P, PROJ_PASSES, CHUNK_DIM], U32, align_bytes=64)
+            w_scales = w_mx_pool.tile([P, PROJ_PASSES, CHUNK_DIM], U8, align_bytes=64)
+            return w_codes, w_scales
+
+        x_codes = const.tile([P, PROJ_PASSES, NEW], U32, align_bytes=64)
+        x_scales = const.tile([P, PROJ_PASSES, NEW], U8, align_bytes=64)
+        weights_mx = {0: new_weights_mx()}
+
+        first_pieces = [
+            (rows_sb, half, g, codes, scales)
+            for rows_sb, (codes, scales) in ((x_sb, (x_codes, x_scales)), (weights_sb[0], weights_mx[0]))
+            for half in range(2)
+            for g in range(PROJ_PASSES)
+        ]
+        waiting = None
+        for number, (rows_sb, half, g, codes, scales) in enumerate(first_pieces):
+            copy = nc.vector.tensor_copy if number % 2 == 0 else nc.scalar.copy
+            grouped = turn_rows(rows_sb, half, g, copy)
+            if waiting is not None:
+                quantise_rows(*waiting)
+            waiting = (grouped, half, g, codes, scales)
+        quantise_rows(*waiting)
+        weights_sb[2] = load_weights(2)
+        weights_sb[3] = load_weights(3)
+
+        sums_of = {}
+        v_new_of = {}
+
+        def project(c, t):
+            w_codes, w_scales = weights_mx[c]
+            tokens = slice(t * P, (t + 1) * P)
+            sums = mx_psum.tile([P, CHUNK_DIM], F32, tag="sums")
+            for g in range(PROJ_PASSES):
+                nc.tensor.matmul_mx(
+                    out=sums[:],
+                    lhsT=x_codes[:, g, tokens].bitcast(FP8X4),
+                    lhsT_scale=x_scales[:, g, tokens],
+                    rhs=w_codes[:, g, :].bitcast(FP8X4),
+                    rhs_scale=w_scales[:, g, :],
+                    start=(g == 0),
+                    stop=(g == PROJ_PASSES - 1),
+                )
+            sums_of[c, t] = sums
+
+        def add_bias(c, t):
+            if t == 0:
+                v_new_of[c] = v_new_pool.tile([P, PACK, CHUNK_DIM], F32, name="v_new")
+            v_new = v_new_of[c]
+            features = slice(c * CHUNK_DIM, (c + 1) * CHUNK_DIM)
+            nc.vector.tensor_tensor(out=v_new[:, t, :], in0=sums_of[c, t][:], in1=bias_bf[:, features], op=ALU.add)
+            nc.sync.dma_start(
+                out=v_new_out[t // 2, t % 2, :, c * CHUNK_HEADS : (c + 1) * CHUNK_HEADS, :],
+                in_=v_new[:, t, :].rearrange("p (h d) -> p h d", d=HEAD_DIM),
+            )
+
+        turned_q = {}
+        turned_k = {}
+
+        def turn_q(h):
+            c, hh = divmod(h, CHUNK_HEADS)
+            q_sb = heads_sb[c][0]
+            q_turned = turned_psum.tile([P, NEW], BF16, tag="turned")
+            for j in range(Q_TILES):
+                nc.tensor.transpose(q_turned[:, j * P : (j + 1) * P], q_sb[:, hh * Q_TILES + j, :], ident_bf[:])
+            q_t = head_pool.tile([P, NEW], BF16)
+            nc.scalar.copy(out=q_t[:], in_=q_turned[:])
+            turned_q[h] = q_t
+
+        def turn_k(h):
+            c, hh = divmod(h, CHUNK_HEADS)
+            k_turned = turned_psum.tile([P, KEYS], BF16, tag="turned")
+            for part, k_sb in enumerate(heads_sb[c][1:3]):
+                for j in range(Q_TILES):
+                    first = part * CACHE + j * P
+                    nc.tensor.transpose(k_turned[:, first : first + P], k_sb[:, hh * Q_TILES + j, :], ident_bf[:])
+            k_t = head_pool.tile([P, KEYS], BF16)
+            nc.scalar.copy(out=k_t[:], in_=k_turned[:])
+            turned_k[h] = k_t
+
+        row_sums_of = {}
+        row_sum_of = {}
+        inverse_of = {}
+        v_grouped_of = {}
+        v_mx = {}
+        ctx_sums_of = {}
+
+        def group_values(h):
+            c, hh = divmod(h, CHUNK_HEADS)
+            v_grouped = head_pool.tile([P, 2, HEAD_DIM, PACK], BF16, align_bytes=64)
+            nc.vector.tensor_copy(out=v_grouped[:, 0], in_=cached_sb[c][:, hh].rearrange("p t d -> p d t"))
+            nc.vector.tensor_copy(
+                out=v_grouped[:, 1],
+                in_=v_new_of[c][:, :, hh * HEAD_DIM : (hh + 1) * HEAD_DIM].rearrange("p t d -> p d t"),
+            )
+            v_grouped_of[h] = v_grouped
+            row_sum = head_pool.tile([P, Q_TILES], F32)
+            nc.vector.tensor_reduce(out=row_sum[:], in_=row_sums_of[h][:], axis=AXIS_X, op=ALU.add)
+            row_sum_of[h] = row_sum
+
+        def quantise_values(h):
+            v_codes = head_pool.tile([P, 2 * HEAD_DIM], U32, align_bytes=64)
+            v_scales = head_pool.tile([P, 2 * HEAD_DIM], U8, align_bytes=64)
+            nc.vector.quantize_mx(
+                out=v_codes[:].bitcast(FP8X4),
+                scales=v_scales[:],
+                in_=v_grouped_of[h][:].rearrange("p a d t -> p (a d t)"),
+            )
+            v_mx[h] = (v_codes, v_scales)
+            inverse = head_pool.tile([P, Q_TILES], F32)
+            nc.vector.reciprocal(out=inverse[:], in_=row_sum_of[h][:])
+            inverse_of[h] = inverse
+
+        def multiply_e_v(h):
+            v_codes, v_scales = v_mx[h]
+            ctx_sums = mx_psum.tile([P, Q_TILES * HEAD_DIM], F32, tag="sums")
+            for i in range(Q_TILES):
+                e_codes, e_scales = e_mx[h * Q_TILES + i]
+                for a in range(2):
+                    columns = slice(a * P, (a + 1) * P)
+                    nc.tensor.matmul_mx(
+                        out=ctx_sums[:, i * HEAD_DIM : (i + 1) * HEAD_DIM],
+                        lhsT=e_codes[:, columns].bitcast(FP8X4),
+                        lhsT_scale=e_scales[:, columns],
+                        rhs=v_codes[:, columns].bitcast(FP8X4),
+                        rhs_scale=v_scales[:, columns],
+                        start=(a == 0),
+                        stop=(a == 1),
+                    )
+            ctx_sums_of[h] = ctx_sums
+
+        def divide_and_store(h):
+            ctx = head_pool.tile([P, Q_TILES, HEAD_DIM], F32)
+            nc.vector.tensor_tensor(
+                out=ctx[:],
+                in0=ctx_sums_of[h][:].rearrange("p (i d) -> p i d", d=HEAD_DIM),
+                in1=inverse_of[h][:].unsqueeze(2).to_broadcast([P, Q_TILES, HEAD_DIM]),
+                op=ALU.mult,
+            )
+            nc.sync.dma_start(
+                out=ctx_out[:, h * HEAD_DIM : (h + 1) * HEAD_DIM].rearrange("(i p) d -> p i d", p=P), in_=ctx[:]
+            )
+
+        scores_of = {}
+        maxima_of = {}
+        shift_of = {}
+        e_grouped_of = {}
+        e_mx = {}
+
+        def scores_and_maxima(n):
+            h, i = divmod(n, Q_TILES)
+            q_t, k_t = turned_q[h], turned_k[h]
+            queries = slice(i * P, (i + 1) * P)
+            before = i * P
+            seen_new = before + P
+            s_cache = score_psum.tile([P, CACHE], F32)
+            nc.tensor.matmul(out=s_cache[:], lhsT=q_t[:, queries], rhs=k_t[:, 0:CACHE], start=True, stop=True)
+            s_new = score_psum.tile([P, NEW], F32)
+            if before > 0:
+                nc.tensor.matmul(
+                    out=s_new[:, 0:before],
+                    lhsT=q_t[:, queries],
+                    rhs=k_t[:, CACHE : CACHE + before],
+                    start=True,
+                    stop=True,
+                )
+            nc.tensor.matmul(
+                out=s_new[:, before:seen_new],
+                lhsT=q_t[:, queries],
+                rhs=k_t[:, CACHE + before : CACHE + seen_new],
+                start=True,
+                stop=False,
+            )
+            nc.tensor.matmul(out=s_new[:, before:seen_new], lhsT=ident_bf[:], rhs=mask_bf[:], start=False, stop=True)
+            maxima = unit_pool.tile([P, 2], F32)
+            nc.vector.tensor_reduce(out=maxima[:, 0:1], in_=s_cache[:], axis=AXIS_X, op=ALU.max)
+            nc.vector.tensor_reduce(out=maxima[:, 1:2], in_=s_new[:, 0:seen_new], axis=AXIS_X, op=ALU.max)
+            scores_of[n] = (s_cache, s_new)
+            maxima_of[n] = maxima
+
+        def shift(n):
+            maxima = maxima_of[n]
+            minus_max = unit_pool.tile([P, 1], F32)
+            nc.vector.tensor_scalar(
+                out=minus_max[:],
+                in0=maxima[:, 0:1],
+                scalar1=maxima[:, 1:2],
+                scalar2=-SCORE_SCALE,
+                op0=ALU.max,
+                op1=ALU.mult,
+            )
+            shift_of[n] = minus_max
+
+        def exponentials(n):
+            h, i = divmod(n, Q_TILES)
+            if i == 0:
+                row_sums_of[h] = head_pool.tile([P, Q_TILES, 2], F32, name="row_sums")
+            s_cache, s_new = scores_of[n]
+            seen_new = (i + 1) * P
+            e_sb = e_rows[i, h % 2]
+            nc.scalar.activation(
+                out=e_sb[:, 0:CACHE],
+                in_=s_cache[:],
+                func=ACT.Exp,
+                bias=shift_of[n][:],
+                scale=SCORE_SCALE,
+                accum_out=row_sums_of[h][:, i, 0:1],
+            )
+            nc.scalar.activation(
+                out=e_sb[:, CACHE : CACHE + seen_new],
+                in_=s_new[:, 0:seen_new],
+                func=ACT.Exp,
+                bias=shift_of[n][:],
+                scale=SCORE_SCALE,
+                accum_out=row_sums_of[h][:, i, 1:2],
+            )
+
+        def turn_e(n):
+            h, i = divmod(n, Q_TILES)
+            e_words = e_rows[i, h % 2][:].bitcast(F32)
+            e_turned = turned_psum.tile([P, 512], F32, tag="turned")
+            for j in range(KEYS // (2 * P)):
+                nc.tensor.transpose(e_turned[:, j * P : (j + 1) * P], e_words[:, j * P : (j + 1) * P], ident_f32[:])
+            e_grouped = unit_pool.tile([P, 2 * P * PACK], BF16, align_bytes=64)
+            nc.scalar.copy(
+                out=e_grouped[:].bitcast(F32).rearrange("p (a m u) -> p a m u", a=2, u=2),
+                in_=e_turned[:].rearrange("p (a u m) -> p a m u", a=2, u=2),
+            )
+            e_grouped_of[n] = e_grouped
+
+        def quantise_e(n):
+            e_codes = e_mx_pool.tile([P, 2 * P], U32, align_bytes=64)
+            e_scales = e_mx_pool.tile([P, 2 * P], U8, align_bytes=64)
+            nc.vector.quantize_mx(out=e_codes[:].bitcast(FP8X4), scales=e_scales[:], in_=e_grouped_of[n][:])
+            e_mx[n] = (e_codes, e_scales)
+
+        def head_that_began(rounds_ago, n):
+            h, i = divmod(n - rounds_ago, Q_TILES)
+            return h if i == 0 and 0 <= h < HEADS else None
+
+        turn_q(0)
+        turn_k(0)
+        weights_piece = None
+        for n in range(ROUNDS):
+            h, i = divmod(n, Q_TILES)
+            c, hh = divmod(h, CHUNK_HEADS)
+            chunk_round = n % UNITS_PER_CHUNK
+
+            if n < UNITS:
+                scores_and_maxima(n)
+            if 0 <= n - QUANTISE_LAG < UNITS:
+                quantise_e(n - QUANTISE_LAG)
+            if n < UNITS:
+                shift(n)
+            if 0 <= n - EXP_LAG < UNITS:
+                exponentials(n - EXP_LAG)
+            if 0 <= n - TURN_LAG < UNITS:
+                turn_e(n - TURN_LAG)
+
+            if weights_piece is not None:
+                quantise_rows(*weights_piece)
+                weights_piece = None
+            if i == 0 and h + 1 < HEADS:
+                turn_q(h + 1)
+            if i == 1 and h + 1 < HEADS:
+                turn_k(h + 1)
+            if i >= 2 and c + 1 < CHUNKS:
+                if hh == 0 and i == 2:
+                    weights_mx[c + 1] = new_weights_mx()
+                grouped = turn_rows(weights_sb[c + 1], i - 2, hh, nc.scalar.copy)
+                weights_piece = (grouped, i - 2, hh) + weights_mx[c + 1]
+
+            if c < CHUNKS and 2 <= chunk_round < 2 + PACK:
+                add_bias(c, chunk_round - 2)
+            if c < CHUNKS and 1 <= chunk_round < 1 + PACK:
+                project(c, chunk_round - 1)
+
+            head = head_that_began(CTX_LAG, n)
+            if head is not None:
+                divide_and_store(head)
+            head = head_that_began(GROUP_V_LAG, n)
+            if head is not None:
+                group_values(head)
+            head = head_that_began(QUANTISE_V_LAG, n)
+            if head is not None:
+                quantise_values(head)
+            head = head_that_began(PV_LAG, n)
+            if head is not None:
+                multiply_e_v(head)
+
+            old, late = divmod(n - RELOAD_LAG, UNITS_PER_CHUNK)
+            if late == 0 and old >= 0 and old + 2 < CHUNKS:
+                heads_sb[old + 2] = load_heads(old + 2)
+                cached_sb[old + 2] = load_cached_values(old + 2)

@@ -252,11 +252,17 @@ def tile_attentionlayer_pa_kernel(tc, q, k_cache, k_new, x, Wv, bv, v_cache, out
         def group_values(h):
             c, hh = divmod(h, CHUNK_HEADS)
             v_grouped = head_pool.tile([P, 2, HEAD_DIM, PACK], BF16, align_bytes=64)
-            nc.vector.tensor_copy(out=v_grouped[:, 0], in_=cached_sb[c][:, hh].rearrange("p t d -> p d t"))
-            nc.vector.tensor_copy(
-                out=v_grouped[:, 1],
-                in_=v_new_of[c][:, :, hh * HEAD_DIM : (hh + 1) * HEAD_DIM].rearrange("p t d -> p d t"),
-            )
+            cached = cached_sb[c][:, hh]
+            new = v_new_of[c][:, :, hh * HEAD_DIM : (hh + 1) * HEAD_DIM]
+            for a, source in enumerate((cached, new)):
+                nc.gpsimd.tensor_scalar(
+                    out=v_grouped[:, a],
+                    in0=source.rearrange("p t d -> p d t"),
+                    scalar1=1.0,
+                    scalar2=0.0,
+                    op0=ALU.mult,
+                    op1=ALU.add,
+                )
             v_grouped_of[h] = v_grouped
             row_sum = head_pool.tile([P, Q_TILES], F32)
             nc.vector.tensor_reduce(out=row_sum[:], in_=row_sums_of[h][:], axis=AXIS_X, op=ALU.add)

@@ -33,16 +33,50 @@ FLOPS = 2 * NEW * DIM * DIM + 2 * (2 * HEADS * NEW * KEYS * HEAD_DIM)
 
 
 UNITS = HEADS * Q_TILES
-UNITS_PER_CHUNK = CHUNK_HEADS * Q_TILES
+TILE_ORDER = (3, 0, 2, 1)
 EXP_LAG = 1
 TURN_LAG = 2
-QUANTISE_LAG = 3
-GROUP_V_LAG = 6
-QUANTISE_V_LAG = 7
+QUANTISE_LAG = 5
+Q_LEAD = 3
+K_LEAD = 2
+FIRST_PIECE_ROUND = 2
+PIECES = 2 * PROJ_PASSES
+SECOND_CHUNK_ROUND = FIRST_PIECE_ROUND + PIECES
+LATER_CHUNK_ROUND = SECOND_CHUNK_ROUND + PIECES + 1
+MX_STEP = 2
+FIRST_PROJECT_ROUND = SECOND_CHUNK_ROUND + 1
 PV_LAG = 8
-CTX_LAG = 9
-RELOAD_LAG = UNITS_PER_CHUNK - Q_TILES + GROUP_V_LAG + 1
-ROUNDS = UNITS - Q_TILES + CTX_LAG + 1
+GROUP_V_LEAD = 3
+ROW_SUM_LEAD = 2
+QUANTISE_V_LEAD = 1
+VECTOR_SHARE = 4
+V_PARTS = 4
+ROUNDS = UNITS - Q_TILES + PV_LAG + 2
+
+
+def unit(n):
+    h, place = divmod(n, Q_TILES)
+    return h, TILE_ORDER[place]
+
+
+def piece_rounds():
+    pieces = {}
+
+    def place(number, source, k):
+        pieces.setdefault(number, []).append((source, k // PROJ_PASSES, k % PROJ_PASSES))
+
+    for k in range(PIECES):
+        place(FIRST_PIECE_ROUND + k // 2, "x", k)
+        place(FIRST_PIECE_ROUND + (PIECES + k) // 2, 0, k)
+        place(SECOND_CHUNK_ROUND + k, 1, k)
+    for c in range(2, CHUNKS):
+        for k in range(PIECES):
+            place(LATER_CHUNK_ROUND + ((c - 2) * PIECES + k) // 2 * Q_TILES + k % 2, c, k)
+    return pieces
+
+
+def last_round(pieces, source):
+    return max(number for number, found in pieces.items() if source in [piece[0] for piece in found])
 
 
 def tile_attentionlayer_pa_kernel(tc, q, k_cache, k_new, x, Wv, bv, v_cache, out_0, out_1):
@@ -65,11 +99,13 @@ def tile_attentionlayer_pa_kernel(tc, q, k_cache, k_new, x, Wv, bv, v_cache, out
         v_new_pool = stack.enter_context(tc.tile_pool(name="v_new", bufs=2))
         grouped_pool = stack.enter_context(tc.tile_pool(name="grouped", bufs=3))
         head_pool = stack.enter_context(tc.tile_pool(name="head", bufs=2))
+        head4_pool = stack.enter_context(tc.tile_pool(name="head4", bufs=6))
         unit_pool = stack.enter_context(tc.tile_pool(name="unit", bufs=4))
-        e_mx_pool = stack.enter_context(tc.tile_pool(name="e_mx", bufs=2 * Q_TILES))
+        e_mx_pool = stack.enter_context(tc.tile_pool(name="e_mx", bufs=5 * Q_TILES))
         score_psum = stack.enter_context(tc.psum_pool(name="score_psum", bufs=2))
         turned_psum = stack.enter_context(tc.psum_pool(name="turned_psum", bufs=2))
-        mx_psum = stack.enter_context(tc.psum_pool(name="mx_psum", bufs=2))
+        e_psum = stack.enter_context(tc.psum_pool(name="e_psum", bufs=1))
+        mx_psum = stack.enter_context(tc.psum_pool(name="mx_psum", bufs=1))
 
         def load_weights(c):
             w_sb = rows_pool.tile([P, PACK, DIM], BF16, tag="rows")
@@ -78,16 +114,18 @@ def tile_attentionlayer_pa_kernel(tc, q, k_cache, k_new, x, Wv, bv, v_cache, out
                 nc.sync.dma_start(out=w_sb[:, a, :], in_=Wv[first : first + P, :])
             return w_sb
 
-        def load_heads(c):
-            first = c * CHUNK_HEADS * NEW
-            rows = slice(first, first + CHUNK_HEADS * NEW)
+        def new_heads():
             q_sb = qkv_pool.tile([P, CHUNK_HEADS * Q_TILES, HEAD_DIM], BF16)
             kc_sb = qkv_pool.tile([P, CHUNK_HEADS * Q_TILES, HEAD_DIM], BF16)
             kn_sb = qkv_pool.tile([P, CHUNK_HEADS * Q_TILES, HEAD_DIM], BF16)
-            nc.sync.dma_start(out=q_sb[:], in_=q_rows[rows, :].rearrange("(j p) d -> p j d", p=P))
-            nc.sync.dma_start(out=kc_sb[:], in_=k_cache_rows[rows, :].rearrange("(j p) d -> p j d", p=P))
-            nc.sync.dma_start(out=kn_sb[:], in_=k_new_rows[rows, :].rearrange("(j p) d -> p j d", p=P))
             return q_sb, kc_sb, kn_sb
+
+        def load_heads(c, tiles, begin, end):
+            first = c * CHUNK_HEADS * NEW
+            rows = slice(first + begin * NEW, first + end * NEW)
+            slots = slice(begin * Q_TILES, end * Q_TILES)
+            for sb, source in zip(tiles, (q_rows, k_cache_rows, k_new_rows)):
+                nc.sync.dma_start(out=sb[:, slots, :], in_=source[rows, :].rearrange("(j p) d -> p j d", p=P))
 
         def load_cached_values(c):
             first = c * CHUNK_HEADS * CACHE
@@ -99,19 +137,24 @@ def tile_attentionlayer_pa_kernel(tc, q, k_cache, k_new, x, Wv, bv, v_cache, out
             )
             return vc_sb
 
+        heads_sb = {0: new_heads()}
+        load_heads(0, heads_sb[0], 0, 1)
         x_sb = rows_pool.tile([P, PACK, DIM], BF16, tag="rows")
         for u in range(2):
             nc.sync.dma_start(
                 out=x_sb[:, 2 * u : 2 * u + 2, :].rearrange("p e k -> p (e k)"),
                 in_=x_rows[256 * u : 256 * u + 256, :].rearrange("(p e) k -> p (e k)", e=2),
             )
+            if u == 0:
+                load_heads(0, heads_sb[0], 1, 2)
         weights_sb = {0: load_weights(0)}
-        heads_sb = {0: load_heads(0)}
+        load_heads(0, heads_sb[0], 2, 4)
         bias_bf = const.tile([P, DIM], BF16)
         nc.sync.dma_start(out=bias_bf[:], in_=bv.partition_broadcast(P))
-        weights_sb[1] = load_weights(1)
         cached_sb = {0: load_cached_values(0)}
-        heads_sb[1] = load_heads(1)
+        weights_sb[1] = load_weights(1)
+        heads_sb[1] = new_heads()
+        load_heads(1, heads_sb[1], 0, 4)
         cached_sb[1] = load_cached_values(1)
 
         warm = const.tile([P, 1], F32)
@@ -169,24 +212,7 @@ def tile_attentionlayer_pa_kernel(tc, q, k_cache, k_new, x, Wv, bv, v_cache, out
 
         x_codes = const.tile([P, PROJ_PASSES, NEW], U32, align_bytes=64)
         x_scales = const.tile([P, PROJ_PASSES, NEW], U8, align_bytes=64)
-        weights_mx = {0: new_weights_mx()}
-
-        first_pieces = [
-            (rows_sb, half, g, codes, scales)
-            for rows_sb, (codes, scales) in ((x_sb, (x_codes, x_scales)), (weights_sb[0], weights_mx[0]))
-            for half in range(2)
-            for g in range(PROJ_PASSES)
-        ]
-        waiting = None
-        for number, (rows_sb, half, g, codes, scales) in enumerate(first_pieces):
-            copy = nc.vector.tensor_copy if number % 2 == 0 else nc.scalar.copy
-            grouped = turn_rows(rows_sb, half, g, copy)
-            if waiting is not None:
-                quantise_rows(*waiting)
-            waiting = (grouped, half, g, codes, scales)
-        quantise_rows(*waiting)
-        weights_sb[2] = load_weights(2)
-        weights_sb[3] = load_weights(3)
+        weights_mx = {}
 
         sums_of = {}
         v_new_of = {}
@@ -228,7 +254,7 @@ def tile_attentionlayer_pa_kernel(tc, q, k_cache, k_new, x, Wv, bv, v_cache, out
             for j in range(Q_TILES):
                 nc.tensor.transpose(q_turned[:, j * P : (j + 1) * P], q_sb[:, hh * Q_TILES + j, :], ident_bf[:])
             q_t = head_pool.tile([P, NEW], BF16)
-            nc.scalar.copy(out=q_t[:], in_=q_turned[:])
+            nc.vector.tensor_copy(out=q_t[:], in_=q_turned[:])
             turned_q[h] = q_t
 
         def turn_k(h):
@@ -249,23 +275,32 @@ def tile_attentionlayer_pa_kernel(tc, q, k_cache, k_new, x, Wv, bv, v_cache, out
         v_mx = {}
         ctx_sums_of = {}
 
-        def group_values(h):
+        def group_values(h, part):
             c, hh = divmod(h, CHUNK_HEADS)
-            v_grouped = head_pool.tile([P, 2, HEAD_DIM, PACK], BF16, align_bytes=64)
-            cached = cached_sb[c][:, hh]
-            new = v_new_of[c][:, :, hh * HEAD_DIM : (hh + 1) * HEAD_DIM]
-            for a, source in enumerate((cached, new)):
+            if part == 0:
+                v_grouped_of[h] = head_pool.tile([P, 2, HEAD_DIM, PACK], BF16, name="v_grouped", align_bytes=64)
+            v_grouped = v_grouped_of[h]
+            width = HEAD_DIM // V_PARTS
+            d0 = part * width
+            for a in range(2):
+                if a == 0:
+                    source = cached_sb[c][:, hh, :, d0 : d0 + width]
+                else:
+                    source = v_new_of[c][:, :, hh * HEAD_DIM + d0 : hh * HEAD_DIM + d0 + width]
                 nc.gpsimd.tensor_scalar(
-                    out=v_grouped[:, a],
+                    out=v_grouped[:, a, d0 : d0 + width],
                     in0=source.rearrange("p t d -> p d t"),
                     scalar1=1.0,
                     scalar2=0.0,
                     op0=ALU.mult,
                     op1=ALU.add,
                 )
-            v_grouped_of[h] = v_grouped
-            row_sum = head_pool.tile([P, Q_TILES], F32)
-            nc.vector.tensor_reduce(out=row_sum[:], in_=row_sums_of[h][:], axis=AXIS_X, op=ALU.add)
+
+        def add_row_sums(h):
+            row_sum = head4_pool.tile([P, Q_TILES], F32)
+            nc.gpsimd.tensor_tensor(
+                out=row_sum[:], in0=row_sums_of[h][:, :, 0], in1=row_sums_of[h][:, :, 1], op=ALU.add
+            )
             row_sum_of[h] = row_sum
 
         def quantise_values(h):
@@ -277,7 +312,7 @@ def tile_attentionlayer_pa_kernel(tc, q, k_cache, k_new, x, Wv, bv, v_cache, out
                 in_=v_grouped_of[h][:].rearrange("p a d t -> p (a d t)"),
             )
             v_mx[h] = (v_codes, v_scales)
-            inverse = head_pool.tile([P, Q_TILES], F32)
+            inverse = head4_pool.tile([P, Q_TILES], F32)
             nc.vector.reciprocal(out=inverse[:], in_=row_sum_of[h][:])
             inverse_of[h] = inverse
 
@@ -285,7 +320,7 @@ def tile_attentionlayer_pa_kernel(tc, q, k_cache, k_new, x, Wv, bv, v_cache, out
             v_codes, v_scales = v_mx[h]
             ctx_sums = mx_psum.tile([P, Q_TILES * HEAD_DIM], F32, tag="sums")
             for i in range(Q_TILES):
-                e_codes, e_scales = e_mx[h * Q_TILES + i]
+                e_codes, e_scales = e_mx[h * Q_TILES + TILE_ORDER.index(i)]
                 for a in range(2):
                     columns = slice(a * P, (a + 1) * P)
                     nc.tensor.matmul_mx(
@@ -317,8 +352,8 @@ def tile_attentionlayer_pa_kernel(tc, q, k_cache, k_new, x, Wv, bv, v_cache, out
         e_grouped_of = {}
         e_mx = {}
 
-        def scores_and_maxima(n):
-            h, i = divmod(n, Q_TILES)
+        def scores(n):
+            h, i = unit(n)
             q_t, k_t = turned_q[h], turned_k[h]
             queries = slice(i * P, (i + 1) * P)
             before = i * P
@@ -342,10 +377,15 @@ def tile_attentionlayer_pa_kernel(tc, q, k_cache, k_new, x, Wv, bv, v_cache, out
                 stop=False,
             )
             nc.tensor.matmul(out=s_new[:, before:seen_new], lhsT=ident_bf[:], rhs=mask_bf[:], start=False, stop=True)
+            scores_of[n] = (s_cache, s_new)
+
+        def find_maxima(n):
+            h, i = unit(n)
+            seen_new = (i + 1) * P
+            s_cache, s_new = scores_of[n]
             maxima = unit_pool.tile([P, 2], F32)
             nc.vector.tensor_reduce(out=maxima[:, 0:1], in_=s_cache[:], axis=AXIS_X, op=ALU.max)
             nc.vector.tensor_reduce(out=maxima[:, 1:2], in_=s_new[:, 0:seen_new], axis=AXIS_X, op=ALU.max)
-            scores_of[n] = (s_cache, s_new)
             maxima_of[n] = maxima
 
         def shift(n):
@@ -362,9 +402,9 @@ def tile_attentionlayer_pa_kernel(tc, q, k_cache, k_new, x, Wv, bv, v_cache, out
             shift_of[n] = minus_max
 
         def exponentials(n):
-            h, i = divmod(n, Q_TILES)
-            if i == 0:
-                row_sums_of[h] = head_pool.tile([P, Q_TILES, 2], F32, name="row_sums")
+            h, i = unit(n)
+            if n % Q_TILES == 0:
+                row_sums_of[h] = head4_pool.tile([P, Q_TILES, 2], F32, name="row_sums")
             s_cache, s_new = scores_of[n]
             seen_new = (i + 1) * P
             e_sb = e_rows[i, h % 2]
@@ -386,9 +426,9 @@ def tile_attentionlayer_pa_kernel(tc, q, k_cache, k_new, x, Wv, bv, v_cache, out
             )
 
         def turn_e(n):
-            h, i = divmod(n, Q_TILES)
+            h, i = unit(n)
             e_words = e_rows[i, h % 2][:].bitcast(F32)
-            e_turned = turned_psum.tile([P, 512], F32, tag="turned")
+            e_turned = e_psum.tile([P, 512], F32)
             for j in range(KEYS // (2 * P)):
                 nc.tensor.transpose(e_turned[:, j * P : (j + 1) * P], e_words[:, j * P : (j + 1) * P], ident_f32[:])
             e_grouped = unit_pool.tile([P, 2 * P * PACK], BF16, align_bytes=64)
@@ -404,22 +444,45 @@ def tile_attentionlayer_pa_kernel(tc, q, k_cache, k_new, x, Wv, bv, v_cache, out
             nc.vector.quantize_mx(out=e_codes[:].bitcast(FP8X4), scales=e_scales[:], in_=e_grouped_of[n][:])
             e_mx[n] = (e_codes, e_scales)
 
-        def head_that_began(rounds_ago, n):
-            h, i = divmod(n - rounds_ago, Q_TILES)
-            return h if i == 0 and 0 <= h < HEADS else None
+        pieces_of_round = piece_rounds()
+        project_of_round = {}
+        ready = {}
+        for c in range(CHUNKS):
+            first = max(FIRST_PROJECT_ROUND + c * PACK * MX_STEP, last_round(pieces_of_round, c) + 1)
+            for t in range(PACK):
+                project_of_round[first + MX_STEP * t] = (c, t)
+            ready[c] = first + MX_STEP * (PACK - 1) + 1
+        pv_rounds = []
+        for h in range(HEADS):
+            earliest = max(Q_TILES * h + PV_LAG, ready[h // CHUNK_HEADS] + GROUP_V_LEAD + 1)
+            pv_rounds.append(max(earliest, pv_rounds[-1] + MX_STEP) if h else earliest)
+        head_of_round = {number: h for h, number in enumerate(pv_rounds)}
 
         turn_q(0)
         turn_k(0)
-        weights_piece = None
+        waiting = []
+        turned_pieces = 0
         for n in range(ROUNDS):
-            h, i = divmod(n, Q_TILES)
-            c, hh = divmod(h, CHUNK_HEADS)
-            chunk_round = n % UNITS_PER_CHUNK
-
             if n < UNITS:
-                scores_and_maxima(n)
+                scores(n)
             if 0 <= n - QUANTISE_LAG < UNITS:
                 quantise_e(n - QUANTISE_LAG)
+            if n - 1 in head_of_round:
+                divide_and_store(head_of_round[n - 1])
+            if n - 1 in project_of_round:
+                add_bias(*project_of_round[n - 1])
+            if n + GROUP_V_LEAD in head_of_round:
+                for part in range(V_PARTS):
+                    group_values(head_of_round[n + GROUP_V_LEAD], part)
+            if n + ROW_SUM_LEAD in head_of_round:
+                add_row_sums(head_of_round[n + ROW_SUM_LEAD])
+            if n < UNITS:
+                find_maxima(n)
+            if n + QUANTISE_V_LEAD in head_of_round:
+                quantise_values(head_of_round[n + QUANTISE_V_LEAD])
+            for piece in waiting:
+                quantise_rows(*piece)
+            waiting = []
             if n < UNITS:
                 shift(n)
             if 0 <= n - EXP_LAG < UNITS:
@@ -427,38 +490,36 @@ def tile_attentionlayer_pa_kernel(tc, q, k_cache, k_new, x, Wv, bv, v_cache, out
             if 0 <= n - TURN_LAG < UNITS:
                 turn_e(n - TURN_LAG)
 
-            if weights_piece is not None:
-                quantise_rows(*weights_piece)
-                weights_piece = None
-            if i == 0 and h + 1 < HEADS:
-                turn_q(h + 1)
-            if i == 1 and h + 1 < HEADS:
-                turn_k(h + 1)
-            if i >= 2 and c + 1 < CHUNKS:
-                if hh == 0 and i == 2:
-                    weights_mx[c + 1] = new_weights_mx()
-                grouped = turn_rows(weights_sb[c + 1], i - 2, hh, nc.scalar.copy)
-                weights_piece = (grouped, i - 2, hh) + weights_mx[c + 1]
+            h, late = divmod(n + Q_LEAD, Q_TILES)
+            if late == 0 and 0 < h < HEADS:
+                turn_q(h)
+            h, late = divmod(n + K_LEAD, Q_TILES)
+            if late == 0 and 0 < h < HEADS:
+                turn_k(h)
+                c, last = divmod(h, CHUNK_HEADS)
+                if last == CHUNK_HEADS - 1 and c + 2 < CHUNKS:
+                    heads_sb[c + 2] = new_heads()
+                    load_heads(c + 2, heads_sb[c + 2], 0, CHUNK_HEADS)
+            for source, half, g in pieces_of_round.get(n, []):
+                if source == "x":
+                    rows_sb, target = x_sb, (x_codes, x_scales)
+                else:
+                    if (half, g) == (0, 0):
+                        weights_mx[source] = new_weights_mx()
+                    rows_sb, target = weights_sb[source], weights_mx[source]
+                copy = nc.scalar.copy if turned_pieces % VECTOR_SHARE else nc.vector.tensor_copy
+                turned_pieces += 1
+                waiting.append((turn_rows(rows_sb, half, g, copy), half, g) + target)
+                if (half, g) == (1, PROJ_PASSES - 1) and source == "x":
+                    weights_sb[2] = load_weights(2)
+                if (half, g) == (1, PROJ_PASSES - 1) and source == 0:
+                    weights_sb[3] = load_weights(3)
 
-            if c < CHUNKS and 2 <= chunk_round < 2 + PACK:
-                add_bias(c, chunk_round - 2)
-            if c < CHUNKS and 1 <= chunk_round < 1 + PACK:
-                project(c, chunk_round - 1)
-
-            head = head_that_began(CTX_LAG, n)
-            if head is not None:
-                divide_and_store(head)
-            head = head_that_began(GROUP_V_LAG, n)
-            if head is not None:
-                group_values(head)
-            head = head_that_began(QUANTISE_V_LAG, n)
-            if head is not None:
-                quantise_values(head)
-            head = head_that_began(PV_LAG, n)
-            if head is not None:
-                multiply_e_v(head)
-
-            old, late = divmod(n - RELOAD_LAG, UNITS_PER_CHUNK)
-            if late == 0 and old >= 0 and old + 2 < CHUNKS:
-                heads_sb[old + 2] = load_heads(old + 2)
-                cached_sb[old + 2] = load_cached_values(old + 2)
+            if n in head_of_round:
+                h = head_of_round[n]
+                multiply_e_v(h)
+                c, last = divmod(h, CHUNK_HEADS)
+                if last == CHUNK_HEADS - 1 and c + 2 < CHUNKS:
+                    cached_sb[c + 2] = load_cached_values(c + 2)
+            if n in project_of_round:
+                project(*project_of_round[n])

@@ -103,9 +103,7 @@ def tile_attentionlayer_pa_kernel(tc, q, k_cache, k_new, x, Wv, bv, v_cache, out
         unit_pool = stack.enter_context(tc.tile_pool(name="unit", bufs=4))
         e_mx_pool = stack.enter_context(tc.tile_pool(name="e_mx", bufs=5 * Q_TILES))
         score_psum = stack.enter_context(tc.psum_pool(name="score_psum", bufs=2))
-        turned_psum = stack.enter_context(tc.psum_pool(name="turned_psum", bufs=2))
-        e_psum = stack.enter_context(tc.psum_pool(name="e_psum", bufs=1))
-        mx_psum = stack.enter_context(tc.psum_pool(name="mx_psum", bufs=1))
+        bank_psum = stack.enter_context(tc.psum_pool(name="bank_psum", bufs=4))
 
         def load_weights(c):
             w_sb = rows_pool.tile([P, PACK, DIM], BF16, tag="rows")
@@ -147,8 +145,8 @@ def tile_attentionlayer_pa_kernel(tc, q, k_cache, k_new, x, Wv, bv, v_cache, out
             )
             if u == 0:
                 load_heads(0, heads_sb[0], 1, 2)
-        weights_sb = {0: load_weights(0)}
         load_heads(0, heads_sb[0], 2, 4)
+        weights_sb = {0: load_weights(0)}
         bias_bf = const.tile([P, DIM], BF16)
         nc.sync.dma_start(out=bias_bf[:], in_=bv.partition_broadcast(P))
         cached_sb = {0: load_cached_values(0)}
@@ -186,7 +184,7 @@ def tile_attentionlayer_pa_kernel(tc, q, k_cache, k_new, x, Wv, bv, v_cache, out
                     nc.vector.memset(e_rows[i, parity][:, seen:KEYS], 0.0)
 
         def turn_rows(rows_sb, half, g, copy):
-            turned = turned_psum.tile([P, 512], F32, tag="turned")
+            turned = bank_psum.tile([P, 512], F32, tag="bank")
             for j in range(2):
                 words = rows_sb[:, 2 * half + j, :].bitcast(F32)
                 for u in range(2):
@@ -220,7 +218,7 @@ def tile_attentionlayer_pa_kernel(tc, q, k_cache, k_new, x, Wv, bv, v_cache, out
         def project(c, t):
             w_codes, w_scales = weights_mx[c]
             tokens = slice(t * P, (t + 1) * P)
-            sums = mx_psum.tile([P, CHUNK_DIM], F32, tag="sums")
+            sums = bank_psum.tile([P, CHUNK_DIM], F32, tag="bank")
             for g in range(PROJ_PASSES):
                 nc.tensor.matmul_mx(
                     out=sums[:],
@@ -250,7 +248,7 @@ def tile_attentionlayer_pa_kernel(tc, q, k_cache, k_new, x, Wv, bv, v_cache, out
         def turn_q(h):
             c, hh = divmod(h, CHUNK_HEADS)
             q_sb = heads_sb[c][0]
-            q_turned = turned_psum.tile([P, NEW], BF16, tag="turned")
+            q_turned = bank_psum.tile([P, NEW], BF16, tag="bank")
             for j in range(Q_TILES):
                 nc.tensor.transpose(q_turned[:, j * P : (j + 1) * P], q_sb[:, hh * Q_TILES + j, :], ident_bf[:])
             q_t = head_pool.tile([P, NEW], BF16)
@@ -259,7 +257,7 @@ def tile_attentionlayer_pa_kernel(tc, q, k_cache, k_new, x, Wv, bv, v_cache, out
 
         def turn_k(h):
             c, hh = divmod(h, CHUNK_HEADS)
-            k_turned = turned_psum.tile([P, KEYS], BF16, tag="turned")
+            k_turned = bank_psum.tile([P, KEYS], BF16, tag="bank")
             for part, k_sb in enumerate(heads_sb[c][1:3]):
                 for j in range(Q_TILES):
                     first = part * CACHE + j * P
@@ -318,7 +316,7 @@ def tile_attentionlayer_pa_kernel(tc, q, k_cache, k_new, x, Wv, bv, v_cache, out
 
         def multiply_e_v(h):
             v_codes, v_scales = v_mx[h]
-            ctx_sums = mx_psum.tile([P, Q_TILES * HEAD_DIM], F32, tag="sums")
+            ctx_sums = bank_psum.tile([P, Q_TILES * HEAD_DIM], F32, tag="bank")
             for i in range(Q_TILES):
                 e_codes, e_scales = e_mx[h * Q_TILES + TILE_ORDER.index(i)]
                 for a in range(2):
@@ -428,7 +426,7 @@ def tile_attentionlayer_pa_kernel(tc, q, k_cache, k_new, x, Wv, bv, v_cache, out
         def turn_e(n):
             h, i = unit(n)
             e_words = e_rows[i, h % 2][:].bitcast(F32)
-            e_turned = e_psum.tile([P, 512], F32)
+            e_turned = bank_psum.tile([P, 512], F32, tag="bank")
             for j in range(KEYS // (2 * P)):
                 nc.tensor.transpose(e_turned[:, j * P : (j + 1) * P], e_words[:, j * P : (j + 1) * P], ident_f32[:])
             e_grouped = unit_pool.tile([P, 2 * P * PACK], BF16, align_bytes=64)

@@ -375,6 +375,14 @@ def tile_attentionlayer_pa_kernel(tc, q, k_cache, k_new, x, Wv, bv, v_cache, out
                 stop=False,
             )
             nc.tensor.matmul(out=s_new[:, before:seen_new], lhsT=ident_bf[:], rhs=mask_bf[:], start=False, stop=True)
+            if seen_new < NEW:
+                nc.tensor.matmul(
+                    out=s_new[:, seen_new:NEW],
+                    lhsT=q_t[:, queries],
+                    rhs=k_t[:, CACHE + seen_new : KEYS],
+                    start=True,
+                    stop=True,
+                )
             scores_of[n] = (s_cache, s_new)
 
         def find_maxima(n):

@@ -39,17 +39,16 @@ TURN_LAG = 2
 QUANTISE_LAG = 5
 Q_LEAD = 3
 K_LEAD = 2
-FIRST_PIECE_ROUND = 2
+FIRST_PIECE_ROUND = 0
 PIECES = 2 * PROJ_PASSES
 SECOND_CHUNK_ROUND = FIRST_PIECE_ROUND + PIECES
-LATER_CHUNK_ROUND = SECOND_CHUNK_ROUND + PIECES + 1
+LATER_CHUNK_ROUND = SECOND_CHUNK_ROUND + PIECES + 3
 MX_STEP = 2
 FIRST_PROJECT_ROUND = SECOND_CHUNK_ROUND + 1
 PV_LAG = 8
 GROUP_V_LEAD = 3
 ROW_SUM_LEAD = 2
 QUANTISE_V_LEAD = 1
-VECTOR_SHARE = 4
 V_PARTS = 4
 ROUNDS = UNITS - Q_TILES + PV_LAG + 2
 
@@ -513,7 +512,8 @@ def tile_attentionlayer_pa_kernel(tc, q, k_cache, k_new, x, Wv, bv, v_cache, out
                     if (half, g) == (0, 0):
                         weights_mx[source] = new_weights_mx()
                     rows_sb, target = weights_sb[source], weights_mx[source]
-                copy = nc.scalar.copy if turned_pieces % VECTOR_SHARE else nc.vector.tensor_copy
+                by_vector = source in ("x", 0, 1) and turned_pieces % 2 == 0
+                copy = nc.vector.tensor_copy if by_vector else nc.scalar.copy
                 turned_pieces += 1
                 waiting.append((turn_rows(rows_sb, half, g, copy), half, g) + target)
                 if (half, g) == (1, PROJ_PASSES - 1) and source == "x":

@@ -49,7 +49,10 @@ PV_LAG = 8
 GROUP_V_LEAD = 3
 ROW_SUM_LEAD = 2
 QUANTISE_V_LEAD = 1
-V_PARTS = 4
+V_PARTS = 2
+CACHED_STEP = 2
+CACHED_LAG = 5
+FIRST_CACHED_ROUND = 9
 ROUNDS = UNITS - Q_TILES + PV_LAG + 2
 
 
@@ -98,18 +101,21 @@ def tile_attentionlayer_pa_kernel(tc, q, k_cache, k_new, x, Wv, bv, v_cache, out
         v_new_pool = stack.enter_context(tc.tile_pool(name="v_new", bufs=2))
         grouped_pool = stack.enter_context(tc.tile_pool(name="grouped", bufs=3))
         head_pool = stack.enter_context(tc.tile_pool(name="head", bufs=2))
+        v_pool = stack.enter_context(tc.tile_pool(name="v", bufs=2))
+        v_mx_pool = stack.enter_context(tc.tile_pool(name="v_mx", bufs=8))
         head4_pool = stack.enter_context(tc.tile_pool(name="head4", bufs=6))
         unit_pool = stack.enter_context(tc.tile_pool(name="unit", bufs=4))
         e_mx_pool = stack.enter_context(tc.tile_pool(name="e_mx", bufs=5 * Q_TILES))
         score_psum = stack.enter_context(tc.psum_pool(name="score_psum", bufs=2))
         bank_psum = stack.enter_context(tc.psum_pool(name="bank_psum", bufs=4))
 
-        def load_weights(c):
-            w_sb = rows_pool.tile([P, PACK, DIM], BF16, tag="rows")
-            for a in range(CHUNK_DIM // P):
+        def new_weights():
+            return rows_pool.tile([P, PACK, DIM], BF16, name="rows", tag="rows")
+
+        def load_weights(c, w_sb, half):
+            for a in range(2 * half, 2 * half + 2):
                 first = c * CHUNK_DIM + a * P
                 nc.sync.dma_start(out=w_sb[:, a, :], in_=Wv[first : first + P, :])
-            return w_sb
 
         def new_heads():
             q_sb = qkv_pool.tile([P, CHUNK_HEADS * Q_TILES, HEAD_DIM], BF16)
@@ -134,25 +140,34 @@ def tile_attentionlayer_pa_kernel(tc, q, k_cache, k_new, x, Wv, bv, v_cache, out
             )
             return vc_sb
 
-        heads_sb = {0: new_heads()}
-        load_heads(0, heads_sb[0], 0, 1)
+        def load_bias(c):
+            features = slice(c * CHUNK_DIM, (c + 1) * CHUNK_DIM)
+            nc.sync.dma_start(out=bias_bf[:, features], in_=bv[features].partition_broadcast(P))
+
+        heads_sb = {0: new_heads(), 1: new_heads()}
         x_sb = rows_pool.tile([P, PACK, DIM], BF16, tag="rows")
+        weights_sb = {0: new_weights(), 1: new_weights()}
+        bias_bf = const.tile([P, DIM], BF16)
         for u in range(2):
+            load_heads(0, heads_sb[0], u, u + 1)
             nc.sync.dma_start(
                 out=x_sb[:, 2 * u : 2 * u + 2, :].rearrange("p e k -> p (e k)"),
                 in_=x_rows[256 * u : 256 * u + 256, :].rearrange("(p e) k -> p (e k)", e=2),
             )
-            if u == 0:
-                load_heads(0, heads_sb[0], 1, 2)
-        load_heads(0, heads_sb[0], 2, 4)
-        weights_sb = {0: load_weights(0)}
-        bias_bf = const.tile([P, DIM], BF16)
-        nc.sync.dma_start(out=bias_bf[:], in_=bv.partition_broadcast(P))
+        load_weights(0, weights_sb[0], 0)
+        load_heads(0, heads_sb[0], 2, 3)
+        load_weights(0, weights_sb[0], 1)
+        load_weights(1, weights_sb[1], 0)
+        load_heads(0, heads_sb[0], 3, 4)
+        load_bias(0)
+        load_weights(1, weights_sb[1], 1)
+        load_heads(1, heads_sb[1], 0, 1)
         cached_sb = {0: load_cached_values(0)}
-        weights_sb[1] = load_weights(1)
-        heads_sb[1] = new_heads()
-        load_heads(1, heads_sb[1], 0, 4)
+        load_bias(1)
+        load_heads(1, heads_sb[1], 1, 4)
         cached_sb[1] = load_cached_values(1)
+        for c in range(2, CHUNKS):
+            load_bias(c)
 
         warm = const.tile([P, 1], F32)
         nc.vector.memset(warm[:], 0.0)
@@ -272,26 +287,27 @@ def tile_attentionlayer_pa_kernel(tc, q, k_cache, k_new, x, Wv, bv, v_cache, out
         v_mx = {}
         ctx_sums_of = {}
 
-        def group_values(h, part):
+        def group_values(h, a, part):
             c, hh = divmod(h, CHUNK_HEADS)
+            if a == 0:
+                source = cached_sb[c][:, hh]
+            else:
+                source = v_new_of[c][:, :, hh * HEAD_DIM : (hh + 1) * HEAD_DIM]
             if part == 0:
-                v_grouped_of[h] = head_pool.tile([P, 2, HEAD_DIM, PACK], BF16, name="v_grouped", align_bytes=64)
-            v_grouped = v_grouped_of[h]
-            width = HEAD_DIM // V_PARTS
-            d0 = part * width
-            for a in range(2):
-                if a == 0:
-                    source = cached_sb[c][:, hh, :, d0 : d0 + width]
-                else:
-                    source = v_new_of[c][:, :, hh * HEAD_DIM + d0 : hh * HEAD_DIM + d0 + width]
-                nc.gpsimd.tensor_scalar(
-                    out=v_grouped[:, a, d0 : d0 + width],
-                    in0=source.rearrange("p t d -> p d t"),
-                    scalar1=1.0,
-                    scalar2=0.0,
-                    op0=ALU.mult,
-                    op1=ALU.add,
-                )
+                v_grouped_of[h, a] = v_pool.tile([P, HEAD_DIM, PACK], BF16, name="v_grouped_%d" % a, align_bytes=64)
+            columns = slice(part * HEAD_DIM // V_PARTS, (part + 1) * HEAD_DIM // V_PARTS)
+            nc.gpsimd.tensor_scalar(
+                out=v_grouped_of[h, a][:, columns],
+                in0=source[:, :, columns].rearrange("p t d -> p d t"),
+                scalar1=1.0,
+                scalar2=0.0,
+                op0=ALU.mult,
+                op1=ALU.add,
+            )
+
+        def wait_for_vector(n):
+            gate = head_pool.tile([P, 1], U32)
+            nc.gpsimd.tensor_copy(out=gate[:], in_=e_mx[n][0][:, 0:1])
 
         def add_row_sums(h):
             row_sum = head4_pool.tile([P, Q_TILES], F32)
@@ -300,15 +316,20 @@ def tile_attentionlayer_pa_kernel(tc, q, k_cache, k_new, x, Wv, bv, v_cache, out
             )
             row_sum_of[h] = row_sum
 
-        def quantise_values(h):
-            v_codes = head_pool.tile([P, 2 * HEAD_DIM], U32, align_bytes=64)
-            v_scales = head_pool.tile([P, 2 * HEAD_DIM], U8, align_bytes=64)
+        def quantise_values(h, a):
+            if a == 0:
+                v_codes = v_mx_pool.tile([P, 2 * HEAD_DIM], U32, align_bytes=64)
+                v_scales = v_mx_pool.tile([P, 2 * HEAD_DIM], U8, align_bytes=64)
+                v_mx[h] = (v_codes, v_scales)
+            v_codes, v_scales = v_mx[h]
+            columns = slice(a * HEAD_DIM, (a + 1) * HEAD_DIM)
             nc.vector.quantize_mx(
-                out=v_codes[:].bitcast(FP8X4),
-                scales=v_scales[:],
-                in_=v_grouped_of[h][:].rearrange("p a d t -> p (a d t)"),
+                out=v_codes[:, columns].bitcast(FP8X4),
+                scales=v_scales[:, columns],
+                in_=v_grouped_of[h, a][:].rearrange("p d t -> p (d t)"),
             )
-            v_mx[h] = (v_codes, v_scales)
+
+        def invert_row_sums(h):
             inverse = head4_pool.tile([P, Q_TILES], F32)
             nc.vector.reciprocal(out=inverse[:], in_=row_sum_of[h][:])
             inverse_of[h] = inverse
@@ -463,6 +484,18 @@ def tile_attentionlayer_pa_kernel(tc, q, k_cache, k_new, x, Wv, bv, v_cache, out
             pv_rounds.append(max(earliest, pv_rounds[-1] + MX_STEP) if h else earliest)
         head_of_round = {number: h for h, number in enumerate(pv_rounds)}
 
+        def reload_weights(c):
+            weights_sb[c] = new_weights()
+            for half in range(2):
+                load_weights(c, weights_sb[c], half)
+
+        cached_rounds = [max(Q_TILES * h + CACHED_LAG, FIRST_CACHED_ROUND + CACHED_STEP * h) for h in range(HEADS)]
+        groups_of_round = {}
+        for h in range(HEADS):
+            for part in range(V_PARTS):
+                groups_of_round.setdefault(cached_rounds[h] - V_PARTS + part, []).append((h, 0, part))
+                groups_of_round.setdefault(pv_rounds[h] - GROUP_V_LEAD + part, []).append((h, 1, part))
+
         turn_q(0)
         turn_k(0)
         waiting = []
@@ -476,15 +509,23 @@ def tile_attentionlayer_pa_kernel(tc, q, k_cache, k_new, x, Wv, bv, v_cache, out
                 divide_and_store(head_of_round[n - 1])
             if n - 1 in project_of_round:
                 add_bias(*project_of_round[n - 1])
-            if n + GROUP_V_LEAD in head_of_round:
-                for part in range(V_PARTS):
-                    group_values(head_of_round[n + GROUP_V_LEAD], part)
+            for h, a, part in groups_of_round.get(n, []):
+                wait_for_vector(n - QUANTISE_LAG)
+                group_values(h, a, part)
+                c, last = divmod(h, CHUNK_HEADS)
+                if (last, a, part) == (CHUNK_HEADS - 1, 0, V_PARTS - 1) and c + 2 < CHUNKS:
+                    cached_sb[c + 2] = load_cached_values(c + 2)
             if n + ROW_SUM_LEAD in head_of_round:
                 add_row_sums(head_of_round[n + ROW_SUM_LEAD])
             if n < UNITS:
                 find_maxima(n)
             if n + QUANTISE_V_LEAD in head_of_round:
-                quantise_values(head_of_round[n + QUANTISE_V_LEAD])
+                h = head_of_round[n + QUANTISE_V_LEAD]
+                quantise_values(h, 1)
+                invert_row_sums(h)
+            for h in range(HEADS):
+                if n == cached_rounds[h]:
+                    quantise_values(h, 0)
             for piece in waiting:
                 quantise_rows(*piece)
             waiting = []
@@ -517,15 +558,12 @@ def tile_attentionlayer_pa_kernel(tc, q, k_cache, k_new, x, Wv, bv, v_cache, out
                 turned_pieces += 1
                 waiting.append((turn_rows(rows_sb, half, g, copy), half, g) + target)
                 if (half, g) == (1, PROJ_PASSES - 1) and source == "x":
-                    weights_sb[2] = load_weights(2)
+                    reload_weights(2)
                 if (half, g) == (1, PROJ_PASSES - 1) and source == 0:
-                    weights_sb[3] = load_weights(3)
+                    reload_weights(3)
 
             if n in head_of_round:
                 h = head_of_round[n]
                 multiply_e_v(h)
-                c, last = divmod(h, CHUNK_HEADS)
-                if last == CHUNK_HEADS - 1 and c + 2 < CHUNKS:
-                    cached_sb[c + 2] = load_cached_values(c + 2)
             if n in project_of_round:
                 project(*project_of_round[n])

@@ -51,9 +51,10 @@ ROW_SUM_LEAD = 2
 QUANTISE_V_LEAD = 1
 V_PARTS = 2
 CACHED_STEP = 2
-CACHED_LAG = 5
+CACHED_LAG = 3
 FIRST_CACHED_ROUND = 9
-ROUNDS = UNITS - Q_TILES + PV_LAG + 2
+LAST_DIVIDE_LAG = 2
+ROUNDS = UNITS + QUANTISE_LAG + LAST_DIVIDE_LAG
 
 
 def unit(n):
@@ -106,6 +107,7 @@ def tile_attentionlayer_pa_kernel(tc, q, k_cache, k_new, x, Wv, bv, v_cache, out
         head4_pool = stack.enter_context(tc.tile_pool(name="head4", bufs=6))
         unit_pool = stack.enter_context(tc.tile_pool(name="unit", bufs=4))
         e_mx_pool = stack.enter_context(tc.tile_pool(name="e_mx", bufs=5 * Q_TILES))
+        ctx_pool = stack.enter_context(tc.tile_pool(name="ctx", bufs=6))
         score_psum = stack.enter_context(tc.psum_pool(name="score_psum", bufs=2))
         bank_psum = stack.enter_context(tc.psum_pool(name="bank_psum", bufs=4))
 
@@ -334,11 +336,12 @@ def tile_attentionlayer_pa_kernel(tc, q, k_cache, k_new, x, Wv, bv, v_cache, out
             nc.vector.reciprocal(out=inverse[:], in_=row_sum_of[h][:])
             inverse_of[h] = inverse
 
-        def multiply_e_v(h):
+        def multiply_e_v(h, units):
             v_codes, v_scales = v_mx[h]
             ctx_sums = bank_psum.tile([P, Q_TILES * HEAD_DIM], F32, tag="bank")
-            for i in range(Q_TILES):
-                e_codes, e_scales = e_mx[h * Q_TILES + TILE_ORDER.index(i)]
+            for n in units:
+                i = unit(n)[1]
+                e_codes, e_scales = e_mx[n]
                 for a in range(2):
                     columns = slice(a * P, (a + 1) * P)
                     nc.tensor.matmul_mx(
@@ -350,18 +353,22 @@ def tile_attentionlayer_pa_kernel(tc, q, k_cache, k_new, x, Wv, bv, v_cache, out
                         start=(a == 0),
                         stop=(a == 1),
                     )
-            ctx_sums_of[h] = ctx_sums
+                ctx_sums_of[h, i] = ctx_sums
 
-        def divide_and_store(h):
-            ctx = head_pool.tile([P, Q_TILES, HEAD_DIM], F32)
+        def divide_and_store(h, first, count):
+            tiles = slice(first, first + count)
+            ctx = ctx_pool.tile([P, Q_TILES, HEAD_DIM], F32)
             nc.vector.tensor_tensor(
-                out=ctx[:],
-                in0=ctx_sums_of[h][:].rearrange("p (i d) -> p i d", d=HEAD_DIM),
-                in1=inverse_of[h][:].unsqueeze(2).to_broadcast([P, Q_TILES, HEAD_DIM]),
+                out=ctx[:, tiles, :],
+                in0=ctx_sums_of[h, first][:].rearrange("p (i d) -> p i d", d=HEAD_DIM)[:, tiles, :],
+                in1=inverse_of[h][:, tiles].unsqueeze(2).to_broadcast([P, count, HEAD_DIM]),
                 op=ALU.mult,
             )
             nc.sync.dma_start(
-                out=ctx_out[:, h * HEAD_DIM : (h + 1) * HEAD_DIM].rearrange("(i p) d -> p i d", p=P), in_=ctx[:]
+                out=ctx_out[first * P : (first + count) * P, h * HEAD_DIM : (h + 1) * HEAD_DIM].rearrange(
+                    "(i p) d -> p i d", p=P
+                ),
+                in_=ctx[:, tiles, :],
             )
 
         scores_of = {}
@@ -482,7 +489,13 @@ def tile_attentionlayer_pa_kernel(tc, q, k_cache, k_new, x, Wv, bv, v_cache, out
         for h in range(HEADS):
             earliest = max(Q_TILES * h + PV_LAG, ready[h // CHUNK_HEADS] + GROUP_V_LEAD + 1)
             pv_rounds.append(max(earliest, pv_rounds[-1] + MX_STEP) if h else earliest)
-        head_of_round = {number: h for h, number in enumerate(pv_rounds)}
+        last_head = HEADS - 1
+        last_units = range(UNITS - Q_TILES, UNITS)
+        head_of_round = {number: h for h, number in enumerate(pv_rounds[:last_head])}
+        pv_rounds[last_head] = last_units[0] + QUANTISE_LAG
+        quantise_of_round = {number - QUANTISE_V_LEAD: h for h, number in enumerate(pv_rounds)}
+        sum_of_round = {number - ROW_SUM_LEAD: h for number, h in head_of_round.items()}
+        sum_of_round[UNITS + EXP_LAG] = last_head
 
         def reload_weights(c):
             weights_sb[c] = new_weights()
@@ -506,7 +519,9 @@ def tile_attentionlayer_pa_kernel(tc, q, k_cache, k_new, x, Wv, bv, v_cache, out
             if 0 <= n - QUANTISE_LAG < UNITS:
                 quantise_e(n - QUANTISE_LAG)
             if n - 1 in head_of_round:
-                divide_and_store(head_of_round[n - 1])
+                divide_and_store(head_of_round[n - 1], 0, Q_TILES)
+            if n - QUANTISE_LAG - LAST_DIVIDE_LAG in last_units:
+                divide_and_store(last_head, unit(n - QUANTISE_LAG - LAST_DIVIDE_LAG)[1], 1)
             if n - 1 in project_of_round:
                 add_bias(*project_of_round[n - 1])
             for h, a, part in groups_of_round.get(n, []):
@@ -515,14 +530,14 @@ def tile_attentionlayer_pa_kernel(tc, q, k_cache, k_new, x, Wv, bv, v_cache, out
                 c, last = divmod(h, CHUNK_HEADS)
                 if (last, a, part) == (CHUNK_HEADS - 1, 0, V_PARTS - 1) and c + 2 < CHUNKS:
                     cached_sb[c + 2] = load_cached_values(c + 2)
-            if n + ROW_SUM_LEAD in head_of_round:
-                add_row_sums(head_of_round[n + ROW_SUM_LEAD])
+            if n in sum_of_round:
+                add_row_sums(sum_of_round[n])
             if n < UNITS:
                 find_maxima(n)
-            if n + QUANTISE_V_LEAD in head_of_round:
-                h = head_of_round[n + QUANTISE_V_LEAD]
-                quantise_values(h, 1)
-                invert_row_sums(h)
+            if n in quantise_of_round:
+                quantise_values(quantise_of_round[n], 1)
+            if n - 1 in sum_of_round:
+                invert_row_sums(sum_of_round[n - 1])
             for h in range(HEADS):
                 if n == cached_rounds[h]:
                     quantise_values(h, 0)
@@ -564,6 +579,8 @@ def tile_attentionlayer_pa_kernel(tc, q, k_cache, k_new, x, Wv, bv, v_cache, out
 
             if n in head_of_round:
                 h = head_of_round[n]
-                multiply_e_v(h)
+                multiply_e_v(h, range(h * Q_TILES, (h + 1) * Q_TILES))
+            if n - QUANTISE_LAG in last_units:
+                multiply_e_v(last_head, [n - QUANTISE_LAG])
             if n in project_of_round:
                 project(*project_of_round[n])

@@ -383,7 +383,10 @@ def tile_attentionlayer_pa_kernel(tc, q, k_cache, k_new, x, Wv, bv, v_cache, out
             queries = slice(i * P, (i + 1) * P)
             before = i * P
             seen_new = before + P
+            keeps_clock = n not in head_of_round and n not in project_of_round
             s_cache = score_psum.tile([P, CACHE], F32)
+            if keeps_clock:
+                nc.tensor.matmul(out=s_cache[:, 0:P], lhsT=q_t[:, queries], rhs=k_t[:, 0:P], start=True, stop=True)
             nc.tensor.matmul(out=s_cache[:], lhsT=q_t[:, queries], rhs=k_t[:, 0:CACHE], start=True, stop=True)
             s_new = score_psum.tile([P, NEW], F32)
             if before > 0:
@@ -402,7 +405,7 @@ def tile_attentionlayer_pa_kernel(tc, q, k_cache, k_new, x, Wv, bv, v_cache, out
                 stop=False,
             )
             nc.tensor.matmul(out=s_new[:, before:seen_new], lhsT=ident_bf[:], rhs=mask_bf[:], start=False, stop=True)
-            if seen_new < NEW:
+            if keeps_clock and seen_new < NEW:
                 nc.tensor.matmul(
                     out=s_new[:, seen_new:NEW],
                     lhsT=q_t[:, queries],

@@ -37,7 +37,7 @@ TILE_ORDER = (3, 0, 2, 1)
 EXP_LAG = 1
 TURN_LAG = 2
 QUANTISE_LAG = 5
-Q_LEAD = 3
+Q_LEAD = 4
 K_LEAD = 2
 FIRST_PIECE_ROUND = 0
 PIECES = 2 * PROJ_PASSES
@@ -100,7 +100,7 @@ def tile_attentionlayer_pa_kernel(tc, q, k_cache, k_new, x, Wv, bv, v_cache, out
         qkv_pool = stack.enter_context(tc.tile_pool(name="qkv", bufs=2))
         w_mx_pool = stack.enter_context(tc.tile_pool(name="w_mx", bufs=2))
         v_new_pool = stack.enter_context(tc.tile_pool(name="v_new", bufs=2))
-        grouped_pool = stack.enter_context(tc.tile_pool(name="grouped", bufs=3))
+        grouped_pool = stack.enter_context(tc.tile_pool(name="grouped", bufs=5))
         head_pool = stack.enter_context(tc.tile_pool(name="head", bufs=2))
         v_pool = stack.enter_context(tc.tile_pool(name="v", bufs=2))
         v_mx_pool = stack.enter_context(tc.tile_pool(name="v_mx", bufs=8))
@@ -515,7 +515,6 @@ def tile_attentionlayer_pa_kernel(tc, q, k_cache, k_new, x, Wv, bv, v_cache, out
         turn_q(0)
         turn_k(0)
         waiting = []
-        turned_pieces = 0
         for n in range(ROUNDS):
             if n < UNITS:
                 scores(n)
@@ -571,9 +570,8 @@ def tile_attentionlayer_pa_kernel(tc, q, k_cache, k_new, x, Wv, bv, v_cache, out
                     if (half, g) == (0, 0):
                         weights_mx[source] = new_weights_mx()
                     rows_sb, target = weights_sb[source], weights_mx[source]
-                by_vector = source in ("x", 0, 1) and turned_pieces % 2 == 0
+                by_vector = source in ("x", 0) and g % 2 == 0
                 copy = nc.vector.tensor_copy if by_vector else nc.scalar.copy
-                turned_pieces += 1
                 waiting.append((turn_rows(rows_sb, half, g, copy), half, g) + target)
                 if (half, g) == (1, PROJ_PASSES - 1) and source == "x":
                     reload_weights(2)

@@ -106,10 +106,9 @@ def tile_attentionlayer_pa_kernel(tc, q, k_cache, k_new, x, Wv, bv, v_cache, out
         v_mx_pool = stack.enter_context(tc.tile_pool(name="v_mx", bufs=8))
         head4_pool = stack.enter_context(tc.tile_pool(name="head4", bufs=6))
         unit_pool = stack.enter_context(tc.tile_pool(name="unit", bufs=4))
-        e_mx_pool = stack.enter_context(tc.tile_pool(name="e_mx", bufs=5 * Q_TILES))
+        e_mx_pool = stack.enter_context(tc.tile_pool(name="e_mx", bufs=10))
         ctx_pool = stack.enter_context(tc.tile_pool(name="ctx", bufs=6))
-        score_psum = stack.enter_context(tc.psum_pool(name="score_psum", bufs=2))
-        bank_psum = stack.enter_context(tc.psum_pool(name="bank_psum", bufs=4))
+        bank_psum = stack.enter_context(tc.psum_pool(name="bank_psum", bufs=8))
 
         def new_weights():
             return rows_pool.tile([P, PACK, DIM], BF16, name="rows", tag="rows")
@@ -384,11 +383,11 @@ def tile_attentionlayer_pa_kernel(tc, q, k_cache, k_new, x, Wv, bv, v_cache, out
             before = i * P
             seen_new = before + P
             keeps_clock = n not in head_of_round and n not in project_of_round
-            s_cache = score_psum.tile([P, CACHE], F32)
+            s_cache = bank_psum.tile([P, CACHE], F32, tag="bank")
             if keeps_clock:
                 nc.tensor.matmul(out=s_cache[:, 0:P], lhsT=q_t[:, queries], rhs=k_t[:, 0:P], start=True, stop=True)
             nc.tensor.matmul(out=s_cache[:], lhsT=q_t[:, queries], rhs=k_t[:, 0:CACHE], start=True, stop=True)
-            s_new = score_psum.tile([P, NEW], F32)
+            s_new = bank_psum.tile([P, NEW], F32, tag="bank")
             if before > 0:
                 nc.tensor.matmul(
                     out=s_new[:, 0:before],
@@ -467,18 +466,34 @@ def tile_attentionlayer_pa_kernel(tc, q, k_cache, k_new, x, Wv, bv, v_cache, out
             e_turned = bank_psum.tile([P, 512], F32, tag="bank")
             for j in range(KEYS // (2 * P)):
                 nc.tensor.transpose(e_turned[:, j * P : (j + 1) * P], e_words[:, j * P : (j + 1) * P], ident_f32[:])
-            e_grouped = unit_pool.tile([P, 2 * P * PACK], BF16, align_bytes=64)
+            if n % 2 == 0 or h == HEADS - 1:
+                units_here = 1 if h == HEADS - 1 else 2
+                e_grouped_of[n] = unit_pool.tile([P, units_here, 2 * P * PACK], BF16, name="e_grouped", align_bytes=64)
+            else:
+                e_grouped_of[n] = e_grouped_of[n - 1]
+            e_grouped = e_grouped_of[n][:, n % 2 if h < HEADS - 1 else 0, :]
             nc.scalar.copy(
-                out=e_grouped[:].bitcast(F32).rearrange("p (a m u) -> p a m u", a=2, u=2),
+                out=e_grouped.bitcast(F32).rearrange("p (a m u) -> p a m u", a=2, u=2),
                 in_=e_turned[:].rearrange("p (a u m) -> p a m u", a=2, u=2),
             )
-            e_grouped_of[n] = e_grouped
 
         def quantise_e(n):
-            e_codes = e_mx_pool.tile([P, 2 * P], U32, align_bytes=64)
-            e_scales = e_mx_pool.tile([P, 2 * P], U8, align_bytes=64)
-            nc.vector.quantize_mx(out=e_codes[:].bitcast(FP8X4), scales=e_scales[:], in_=e_grouped_of[n][:])
-            e_mx[n] = (e_codes, e_scales)
+            pair = n < UNITS - Q_TILES
+            if pair and n % 2 == 0:
+                return
+            width = 4 * P if pair else 2 * P
+            e_codes = e_mx_pool.tile([P, width], U32, name="e_codes", align_bytes=64)
+            e_scales = e_mx_pool.tile([P, width], U8, name="e_scales", align_bytes=64)
+            nc.vector.quantize_mx(
+                out=e_codes[:].bitcast(FP8X4),
+                scales=e_scales[:],
+                in_=e_grouped_of[n][:].rearrange("p n w -> p (n w)"),
+            )
+            if pair:
+                e_mx[n - 1] = (e_codes[:, 0 : 2 * P], e_scales[:, 0 : 2 * P])
+                e_mx[n] = (e_codes[:, 2 * P : 4 * P], e_scales[:, 2 * P : 4 * P])
+            else:
+                e_mx[n] = (e_codes[:], e_scales[:])
 
         pieces_of_round = piece_rounds()
         project_of_round = {}
@@ -527,7 +542,7 @@ def tile_attentionlayer_pa_kernel(tc, q, k_cache, k_new, x, Wv, bv, v_cache, out
             if n - 1 in project_of_round:
                 add_bias(*project_of_round[n - 1])
             for h, a, part in groups_of_round.get(n, []):
-                wait_for_vector(n - QUANTISE_LAG)
+                wait_for_vector((n - QUANTISE_LAG - 1) // 2 * 2 + 1)
                 group_values(h, a, part)
                 c, last = divmod(h, CHUNK_HEADS)
                 if (last, a, part) == (CHUNK_HEADS - 1, 0, V_PARTS - 1) and c + 2 < CHUNKS:

@@ -35,7 +35,8 @@ FLOPS = 2 * NEW * DIM * DIM + 2 * (2 * HEADS * NEW * KEYS * HEAD_DIM)
 UNITS = HEADS * Q_TILES
 TILE_ORDER = (3, 0, 2, 1)
 EXP_LAG = 1
-TURN_LAG = 2
+TURN_LAG = 3
+LAST_TURN_LAG = 2
 QUANTISE_LAG = 5
 Q_LEAD = 4
 K_LEAD = 2
@@ -52,7 +53,7 @@ QUANTISE_V_LEAD = 1
 V_PARTS = 2
 CACHED_STEP = 2
 CACHED_LAG = 3
-FIRST_CACHED_ROUND = 9
+FIRST_CACHED_ROUND = 14
 LAST_DIVIDE_LAG = 2
 ROUNDS = UNITS + QUANTISE_LAG + LAST_DIVIDE_LAG
 
@@ -106,7 +107,7 @@ def tile_attentionlayer_pa_kernel(tc, q, k_cache, k_new, x, Wv, bv, v_cache, out
         v_mx_pool = stack.enter_context(tc.tile_pool(name="v_mx", bufs=8))
         head4_pool = stack.enter_context(tc.tile_pool(name="head4", bufs=6))
         unit_pool = stack.enter_context(tc.tile_pool(name="unit", bufs=4))
-        e_mx_pool = stack.enter_context(tc.tile_pool(name="e_mx", bufs=10))
+        e_mx_pool = stack.enter_context(tc.tile_pool(name="e_mx", bufs=5 * Q_TILES))
         ctx_pool = stack.enter_context(tc.tile_pool(name="ctx", bufs=6))
         bank_psum = stack.enter_context(tc.psum_pool(name="bank_psum", bufs=8))
 
@@ -141,16 +142,18 @@ def tile_attentionlayer_pa_kernel(tc, q, k_cache, k_new, x, Wv, bv, v_cache, out
             )
             return vc_sb
 
-        def load_bias(c):
-            features = slice(c * CHUNK_DIM, (c + 1) * CHUNK_DIM)
-            nc.sync.dma_start(out=bias_bf[:, features], in_=bv[features].partition_broadcast(P))
-
+        zeros = const.tile([P, CACHE], BF16)
+        nc.vector.memset(zeros[:], 0.0)
+        bias_rows = v_new_pool.tile([P, DIM], BF16, name="bias_rows", tag="v_new")
+        nc.vector.memset(bias_rows[:], 0.0)
         heads_sb = {0: new_heads(), 1: new_heads()}
         x_sb = rows_pool.tile([P, PACK, DIM], BF16, tag="rows")
         weights_sb = {0: new_weights(), 1: new_weights()}
         bias_bf = const.tile([P, DIM], BF16)
         for u in range(2):
             load_heads(0, heads_sb[0], u, u + 1)
+            if u == 0:
+                nc.sync.dma_start(out=bias_rows[0:1, :], in_=bv.rearrange("(o f) -> o f", o=1))
             nc.sync.dma_start(
                 out=x_sb[:, 2 * u : 2 * u + 2, :].rearrange("p e k -> p (e k)"),
                 in_=x_rows[256 * u : 256 * u + 256, :].rearrange("(p e) k -> p (e k)", e=2),
@@ -160,36 +163,32 @@ def tile_attentionlayer_pa_kernel(tc, q, k_cache, k_new, x, Wv, bv, v_cache, out
         load_weights(0, weights_sb[0], 1)
         load_weights(1, weights_sb[1], 0)
         load_heads(0, heads_sb[0], 3, 4)
-        load_bias(0)
         load_weights(1, weights_sb[1], 1)
         load_heads(1, heads_sb[1], 0, 1)
         cached_sb = {0: load_cached_values(0)}
-        load_bias(1)
         load_heads(1, heads_sb[1], 1, 4)
         cached_sb[1] = load_cached_values(1)
-        for c in range(2, CHUNKS):
-            load_bias(c)
 
         warm = const.tile([P, 1], F32)
         nc.vector.memset(warm[:], 0.0)
         nc.scalar.activation(out=warm[:], in_=warm[:], func=ACT.Exp)
-        ident_f32 = const.tile([P, P], F32)
-        make_identity(nc, ident_f32[:])
+        ones = const.tile([P, P], BF16)
+        nc.vector.memset(ones[:], 1.0)
         ident_bf = const.tile([P, P], BF16)
         make_identity(nc, ident_bf[:])
-        mask_f32 = const.tile([P, P], F32)
-        nc.gpsimd.memset(mask_f32[:], 0.0)
+        mask_bf = const.tile([P, P], BF16)
+        nc.gpsimd.memset(mask_bf[:], 0.0)
         nc.gpsimd.affine_select(
-            out=mask_f32[:],
-            in_=mask_f32[:],
+            out=mask_bf[:],
+            in_=mask_bf[:],
             pattern=[[-1, P]],
             compare_op=ALU.is_ge,
             fill=MASKED,
             base=0,
             channel_multiplier=1,
         )
-        mask_bf = const.tile([P, P], BF16)
-        nc.vector.tensor_copy(out=mask_bf[:], in_=mask_f32[:])
+        ident_f32 = const.tile([P, P], F32)
+        make_identity(nc, ident_f32[:])
         e_rows = {}
         for i in range(Q_TILES):
             for parity in range(2):
@@ -248,7 +247,7 @@ def tile_attentionlayer_pa_kernel(tc, q, k_cache, k_new, x, Wv, bv, v_cache, out
 
         def add_bias(c, t):
             if t == 0:
-                v_new_of[c] = v_new_pool.tile([P, PACK, CHUNK_DIM], F32, name="v_new")
+                v_new_of[c] = v_new_pool.tile([P, PACK, CHUNK_DIM], F32, name="v_new", tag="v_new")
             v_new = v_new_of[c]
             features = slice(c * CHUNK_DIM, (c + 1) * CHUNK_DIM)
             nc.vector.tensor_tensor(out=v_new[:, t, :], in0=sums_of[c, t][:], in1=bias_bf[:, features], op=ALU.add)
@@ -305,10 +304,6 @@ def tile_attentionlayer_pa_kernel(tc, q, k_cache, k_new, x, Wv, bv, v_cache, out
                 op0=ALU.mult,
                 op1=ALU.add,
             )
-
-        def wait_for_vector(n):
-            gate = head_pool.tile([P, 1], U32)
-            nc.gpsimd.tensor_copy(out=gate[:], in_=e_mx[n][0][:, 0:1])
 
         def add_row_sums(h):
             row_sum = head4_pool.tile([P, Q_TILES], F32)
@@ -388,30 +383,15 @@ def tile_attentionlayer_pa_kernel(tc, q, k_cache, k_new, x, Wv, bv, v_cache, out
                 nc.tensor.matmul(out=s_cache[:, 0:P], lhsT=q_t[:, queries], rhs=k_t[:, 0:P], start=True, stop=True)
             nc.tensor.matmul(out=s_cache[:], lhsT=q_t[:, queries], rhs=k_t[:, 0:CACHE], start=True, stop=True)
             s_new = bank_psum.tile([P, NEW], F32, tag="bank")
-            if before > 0:
-                nc.tensor.matmul(
-                    out=s_new[:, 0:before],
-                    lhsT=q_t[:, queries],
-                    rhs=k_t[:, CACHE : CACHE + before],
-                    start=True,
-                    stop=True,
-                )
+            width = NEW if keeps_clock else seen_new
             nc.tensor.matmul(
-                out=s_new[:, before:seen_new],
+                out=s_new[:, 0:width],
                 lhsT=q_t[:, queries],
-                rhs=k_t[:, CACHE + before : CACHE + seen_new],
+                rhs=k_t[:, CACHE : CACHE + width],
                 start=True,
                 stop=False,
             )
             nc.tensor.matmul(out=s_new[:, before:seen_new], lhsT=ident_bf[:], rhs=mask_bf[:], start=False, stop=True)
-            if keeps_clock and seen_new < NEW:
-                nc.tensor.matmul(
-                    out=s_new[:, seen_new:NEW],
-                    lhsT=q_t[:, queries],
-                    rhs=k_t[:, CACHE + seen_new : KEYS],
-                    start=True,
-                    stop=True,
-                )
             scores_of[n] = (s_cache, s_new)
 
         def find_maxima(n):
@@ -466,34 +446,18 @@ def tile_attentionlayer_pa_kernel(tc, q, k_cache, k_new, x, Wv, bv, v_cache, out
             e_turned = bank_psum.tile([P, 512], F32, tag="bank")
             for j in range(KEYS // (2 * P)):
                 nc.tensor.transpose(e_turned[:, j * P : (j + 1) * P], e_words[:, j * P : (j + 1) * P], ident_f32[:])
-            if n % 2 == 0 or h == HEADS - 1:
-                units_here = 1 if h == HEADS - 1 else 2
-                e_grouped_of[n] = unit_pool.tile([P, units_here, 2 * P * PACK], BF16, name="e_grouped", align_bytes=64)
-            else:
-                e_grouped_of[n] = e_grouped_of[n - 1]
-            e_grouped = e_grouped_of[n][:, n % 2 if h < HEADS - 1 else 0, :]
+            e_grouped = unit_pool.tile([P, 2 * P * PACK], BF16, align_bytes=64)
             nc.scalar.copy(
-                out=e_grouped.bitcast(F32).rearrange("p (a m u) -> p a m u", a=2, u=2),
+                out=e_grouped[:].bitcast(F32).rearrange("p (a m u) -> p a m u", a=2, u=2),
                 in_=e_turned[:].rearrange("p (a u m) -> p a m u", a=2, u=2),
             )
+            e_grouped_of[n] = e_grouped
 
         def quantise_e(n):
-            pair = n < UNITS - Q_TILES
-            if pair and n % 2 == 0:
-                return
-            width = 4 * P if pair else 2 * P
-            e_codes = e_mx_pool.tile([P, width], U32, name="e_codes", align_bytes=64)
-            e_scales = e_mx_pool.tile([P, width], U8, name="e_scales", align_bytes=64)
-            nc.vector.quantize_mx(
-                out=e_codes[:].bitcast(FP8X4),
-                scales=e_scales[:],
-                in_=e_grouped_of[n][:].rearrange("p n w -> p (n w)"),
-            )
-            if pair:
-                e_mx[n - 1] = (e_codes[:, 0 : 2 * P], e_scales[:, 0 : 2 * P])
-                e_mx[n] = (e_codes[:, 2 * P : 4 * P], e_scales[:, 2 * P : 4 * P])
-            else:
-                e_mx[n] = (e_codes[:], e_scales[:])
+            e_codes = e_mx_pool.tile([P, 2 * P], U32, align_bytes=64)
+            e_scales = e_mx_pool.tile([P, 2 * P], U8, align_bytes=64)
+            nc.vector.quantize_mx(out=e_codes[:].bitcast(FP8X4), scales=e_scales[:], in_=e_grouped_of[n][:])
+            e_mx[n] = (e_codes, e_scales)
 
         pieces_of_round = piece_rounds()
         project_of_round = {}
@@ -527,13 +491,25 @@ def tile_attentionlayer_pa_kernel(tc, q, k_cache, k_new, x, Wv, bv, v_cache, out
                 groups_of_round.setdefault(cached_rounds[h] - V_PARTS + part, []).append((h, 0, part))
                 groups_of_round.setdefault(pv_rounds[h] - GROUP_V_LEAD + part, []).append((h, 1, part))
 
+        def spread_bias(c, copy):
+            features = slice(c * CHUNK_DIM, (c + 1) * CHUNK_DIM)
+            spread = bank_psum.tile([P, CHUNK_DIM], F32, name="spread", tag="bank")
+            nc.tensor.matmul(out=spread[:], lhsT=ones[:], rhs=bias_rows[:, features], start=True, stop=True)
+            copy(out=bias_bf[:, features], in_=spread[:])
+
+        unread = bank_psum.tile([P, CACHE], F32, name="unread", tag="bank")
+        for i in range(4):
+            nc.tensor.matmul(out=unread[:], lhsT=zeros[:, 0:P], rhs=zeros[:], start=True, stop=True)
         turn_q(0)
         turn_k(0)
+        for c in range(CHUNKS):
+            spread_bias(c, nc.vector.tensor_copy if c % 2 == 0 else nc.scalar.copy)
         waiting = []
         for n in range(ROUNDS):
             if n < UNITS:
                 scores(n)
-            if 0 <= n - QUANTISE_LAG < UNITS:
+            between = bool(waiting) or n in quantise_of_round or n in cached_rounds
+            if between and 0 <= n - QUANTISE_LAG < UNITS:
                 quantise_e(n - QUANTISE_LAG)
             if n - 1 in head_of_round:
                 divide_and_store(head_of_round[n - 1], 0, Q_TILES)
@@ -542,7 +518,6 @@ def tile_attentionlayer_pa_kernel(tc, q, k_cache, k_new, x, Wv, bv, v_cache, out
             if n - 1 in project_of_round:
                 add_bias(*project_of_round[n - 1])
             for h, a, part in groups_of_round.get(n, []):
-                wait_for_vector((n - QUANTISE_LAG - 1) // 2 * 2 + 1)
                 group_values(h, a, part)
                 c, last = divmod(h, CHUNK_HEADS)
                 if (last, a, part) == (CHUNK_HEADS - 1, 0, V_PARTS - 1) and c + 2 < CHUNKS:
@@ -551,6 +526,8 @@ def tile_attentionlayer_pa_kernel(tc, q, k_cache, k_new, x, Wv, bv, v_cache, out
                 add_row_sums(sum_of_round[n])
             if n < UNITS:
                 find_maxima(n)
+            if not between and 0 <= n - QUANTISE_LAG < UNITS:
+                quantise_e(n - QUANTISE_LAG)
             if n in quantise_of_round:
                 quantise_values(quantise_of_round[n], 1)
             if n - 1 in sum_of_round:
@@ -565,8 +542,10 @@ def tile_attentionlayer_pa_kernel(tc, q, k_cache, k_new, x, Wv, bv, v_cache, out
                 shift(n)
             if 0 <= n - EXP_LAG < UNITS:
                 exponentials(n - EXP_LAG)
-            if 0 <= n - TURN_LAG < UNITS:
+            if 0 <= n - TURN_LAG < UNITS - 2:
                 turn_e(n - TURN_LAG)
+            if n - LAST_TURN_LAG in (UNITS - 2, UNITS - 1):
+                turn_e(n - LAST_TURN_LAG)
 
             h, late = divmod(n + Q_LEAD, Q_TILES)
             if late == 0 and 0 < h < HEADS:

from contextlib import ExitStack

import concourse.mybir as mybir
from concourse.masks import make_identity

BF16 = mybir.dt.bfloat16
F32 = mybir.dt.float32
U32 = mybir.dt.uint32
U8 = mybir.dt.uint8
FP8X4 = mybir.dt.float8_e4m3fn_x4
ALU = mybir.AluOpType
ACT = mybir.ActivationFunctionType
AXIS_X = mybir.AxisListType.X

P = 128
PACK = 4
K_PASS = P * PACK
HEADS = 16
HEAD_DIM = 128
NEW = 512
CACHE = 512
KEYS = CACHE + NEW
DIM = HEADS * HEAD_DIM
Q_TILES = NEW // P
PROJ_PASSES = DIM // K_PASS
CHUNK_HEADS = 4
CHUNKS = HEADS // CHUNK_HEADS
CHUNK_DIM = CHUNK_HEADS * HEAD_DIM
SCORE_SCALE = 1.0 / (HEAD_DIM**0.5)
MASKED = -1.0e30

FLOPS = 2 * NEW * DIM * DIM + 2 * (2 * HEADS * NEW * KEYS * HEAD_DIM)


UNITS = HEADS * Q_TILES
TILE_ORDER = (3, 0, 2, 1)
EXP_LAG = 1
TURN_LAG = 3
LAST_TURN_LAG = 2
QUANTISE_LAG = 5
Q_LEAD = 4
K_LEAD = 2
FIRST_PIECE_ROUND = 0
PIECES = 2 * PROJ_PASSES
SECOND_CHUNK_ROUND = FIRST_PIECE_ROUND + PIECES
LATER_CHUNK_ROUND = SECOND_CHUNK_ROUND + PIECES + 3
MX_STEP = 2
FIRST_PROJECT_ROUND = SECOND_CHUNK_ROUND + 1
PV_LAG = 8
GROUP_V_LEAD = 3
ROW_SUM_LEAD = 2
QUANTISE_V_LEAD = 1
V_PARTS = 2
CACHED_STEP = 2
CACHED_LAG = 3
FIRST_CACHED_ROUND = 14
LAST_DIVIDE_LAG = 2
ROUNDS = UNITS + QUANTISE_LAG + LAST_DIVIDE_LAG


def unit(n):
    h, place = divmod(n, Q_TILES)
    return h, TILE_ORDER[place]


def piece_rounds():
    pieces = {}

    def place(number, source, k):
        pieces.setdefault(number, []).append((source, k // PROJ_PASSES, k % PROJ_PASSES))

    for k in range(PIECES):
        place(FIRST_PIECE_ROUND + k // 2, "x", k)
        place(FIRST_PIECE_ROUND + (PIECES + k) // 2, 0, k)
        place(SECOND_CHUNK_ROUND + k, 1, k)
    for c in range(2, CHUNKS):
        for k in range(PIECES):
            place(LATER_CHUNK_ROUND + ((c - 2) * PIECES + k) // 2 * Q_TILES + k % 2, c, k)
    return pieces


def last_round(pieces, source):
    return max(number for number, found in pieces.items() if source in [piece[0] for piece in found])


def tile_attentionlayer_pa_kernel(tc, q, k_cache, k_new, x, Wv, bv, v_cache, out_0, out_1):
    nc = tc.nc

    q_rows = q.rearrange("b h s d -> (b h s) d")
    k_cache_rows = k_cache.rearrange("b h s d -> (b h s) d")
    k_new_rows = k_new.rearrange("b h s d -> (b h s) d")
    v_cache_rows = v_cache.rearrange("b h s d -> (b h s) d")
    x_rows = x.rearrange("b s k -> (b s) k")
    ctx_out = out_0.rearrange("b s f -> (b s) f")
    v_new_out = out_1.rearrange("b h s d -> (b h) s d").rearrange("h (u p e) d -> u e p h d", u=2, e=2)

    with ExitStack() as stack:
        stack.enter_context(tc.manual_schedule())
        const = stack.enter_context(tc.tile_pool(name="const", bufs=1))
        rows_pool = stack.enter_context(tc.tile_pool(name="rows", bufs=3))
        qkv_pool = stack.enter_context(tc.tile_pool(name="qkv", bufs=2))
        w_mx_pool = stack.enter_context(tc.tile_pool(name="w_mx", bufs=2))
        v_new_pool = stack.enter_context(tc.tile_pool(name="v_new", bufs=2))
        grouped_pool = stack.enter_context(tc.tile_pool(name="grouped", bufs=5))
        head_pool = stack.enter_context(tc.tile_pool(name="head", bufs=2))
        v_pool = stack.enter_context(tc.tile_pool(name="v", bufs=2))
        v_mx_pool = stack.enter_context(tc.tile_pool(name="v_mx", bufs=8))
        head4_pool = stack.enter_context(tc.tile_pool(name="head4", bufs=6))
        unit_pool = stack.enter_context(tc.tile_pool(name="unit", bufs=4))
        e_mx_pool = stack.enter_context(tc.tile_pool(name="e_mx", bufs=5 * Q_TILES))
        ctx_pool = stack.enter_context(tc.tile_pool(name="ctx", bufs=6))
        bank_psum = stack.enter_context(tc.psum_pool(name="bank_psum", bufs=8))

        def new_weights():
            return rows_pool.tile([P, PACK, DIM], BF16, name="rows", tag="rows")

        def load_weights(c, w_sb, half):
            for a in range(2 * half, 2 * half + 2):
                first = c * CHUNK_DIM + a * P
                nc.sync.dma_start(out=w_sb[:, a, :], in_=Wv[first : first + P, :])

        def new_heads():
            q_sb = qkv_pool.tile([P, CHUNK_HEADS * Q_TILES, HEAD_DIM], BF16)
            kc_sb = qkv_pool.tile([P, CHUNK_HEADS * Q_TILES, HEAD_DIM], BF16)
            kn_sb = qkv_pool.tile([P, CHUNK_HEADS * Q_TILES, HEAD_DIM], BF16)
            return q_sb, kc_sb, kn_sb

        def load_heads(c, tiles, begin, end):
            first = c * CHUNK_HEADS * NEW
            rows = slice(first + begin * NEW, first + end * NEW)
            slots = slice(begin * Q_TILES, end * Q_TILES)
            for sb, source in zip(tiles, (q_rows, k_cache_rows, k_new_rows)):
                nc.sync.dma_start(out=sb[:, slots, :], in_=source[rows, :].rearrange("(j p) d -> p j d", p=P))

        def load_cached_values(c):
            first = c * CHUNK_HEADS * CACHE
            rows = slice(first, first + CHUNK_HEADS * CACHE)
            vc_sb = qkv_pool.tile([P, CHUNK_HEADS, PACK, HEAD_DIM], BF16)
            nc.sync.dma_start(
                out=vc_sb[:].rearrange("p h (u e) d -> p (h u) (e d)", e=2),
                in_=v_cache_rows[rows, :].rearrange("(hu p e) d -> p hu (e d)", p=P, e=2),
            )
            return vc_sb

        zeros = const.tile([P, CACHE], BF16)
        nc.vector.memset(zeros[:], 0.0)
        bias_rows = v_new_pool.tile([P, DIM], BF16, name="bias_rows", tag="v_new")
        nc.vector.memset(bias_rows[:], 0.0)
        heads_sb = {0: new_heads(), 1: new_heads()}
        x_sb = rows_pool.tile([P, PACK, DIM], BF16, tag="rows")
        weights_sb = {0: new_weights(), 1: new_weights()}
        bias_bf = const.tile([P, DIM], BF16)
        for u in range(2):
            load_heads(0, heads_sb[0], u, u + 1)
            if u == 0:
                nc.sync.dma_start(out=bias_rows[0:1, :], in_=bv.rearrange("(o f) -> o f", o=1))
            nc.sync.dma_start(
                out=x_sb[:, 2 * u : 2 * u + 2, :].rearrange("p e k -> p (e k)"),
                in_=x_rows[256 * u : 256 * u + 256, :].rearrange("(p e) k -> p (e k)", e=2),
            )
        load_weights(0, weights_sb[0], 0)
        load_heads(0, heads_sb[0], 2, 3)
        load_weights(0, weights_sb[0], 1)
        load_weights(1, weights_sb[1], 0)
        load_heads(0, heads_sb[0], 3, 4)
        load_weights(1, weights_sb[1], 1)
        load_heads(1, heads_sb[1], 0, 1)
        cached_sb = {0: load_cached_values(0)}
        load_heads(1, heads_sb[1], 1, 4)
        cached_sb[1] = load_cached_values(1)

        warm = const.tile([P, 1], F32)
        nc.vector.memset(warm[:], 0.0)
        nc.scalar.activation(out=warm[:], in_=warm[:], func=ACT.Exp)
        ones = const.tile([P, P], BF16)
        nc.vector.memset(ones[:], 1.0)
        ident_bf = const.tile([P, P], BF16)
        make_identity(nc, ident_bf[:])
        mask_bf = const.tile([P, P], BF16)
        nc.gpsimd.memset(mask_bf[:], 0.0)
        nc.gpsimd.affine_select(
            out=mask_bf[:],
            in_=mask_bf[:],
            pattern=[[-1, P]],
            compare_op=ALU.is_ge,
            fill=MASKED,
            base=0,
            channel_multiplier=1,
        )
        ident_f32 = const.tile([P, P], F32)
        make_identity(nc, ident_f32[:])
        e_rows = {}
        for i in range(Q_TILES):
            for parity in range(2):
                e_rows[i, parity] = const.tile([P, KEYS], BF16, name="e_rows_%d_%d" % (i, parity))
                seen = CACHE + (i + 1) * P
                if seen < KEYS:
                    nc.vector.memset(e_rows[i, parity][:, seen:KEYS], 0.0)

        def turn_rows(rows_sb, half, g, copy):
            turned = bank_psum.tile([P, 512], F32, tag="bank")
            for j in range(2):
                words = rows_sb[:, 2 * half + j, :].bitcast(F32)
                for u in range(2):
                    first = (K_PASS // 2) * g + P * u
                    nc.tensor.transpose(
                        turned[:, (2 * j + u) * P : (2 * j + u + 1) * P], words[:, first : first + P], ident_f32[:]
                    )
            grouped = grouped_pool.tile([P, 2 * P * PACK], BF16, tag="grouped", align_bytes=64)
            copy(
                out=grouped[:].bitcast(F32).rearrange("p (j m u) -> p j m u", j=2, u=2),
                in_=turned[:].rearrange("p (j u m) -> p j m u", j=2, u=2),
            )
            return grouped

        def quantise_rows(grouped, half, g, codes, scales):
            columns = slice(2 * P * half, 2 * P * (half + 1))
            nc.vector.quantize_mx(out=codes[:, g, columns].bitcast(FP8X4), scales=scales[:, g, columns], in_=grouped[:])

        def new_weights_mx():
            w_codes = w_mx_pool.tile([P, PROJ_PASSES, CHUNK_DIM], U32, align_bytes=64)
            w_scales = w_mx_pool.tile([P, PROJ_PASSES, CHUNK_DIM], U8, align_bytes=64)
            return w_codes, w_scales

        x_codes = const.tile([P, PROJ_PASSES, NEW], U32, align_bytes=64)
        x_scales = const.tile([P, PROJ_PASSES, NEW], U8, align_bytes=64)
        weights_mx = {}

        sums_of = {}
        v_new_of = {}

        def project(c, t):
            w_codes, w_scales = weights_mx[c]
            tokens = slice(t * P, (t + 1) * P)
            sums = bank_psum.tile([P, CHUNK_DIM], F32, tag="bank")
            for g in range(PROJ_PASSES):
                nc.tensor.matmul_mx(
                    out=sums[:],
                    lhsT=x_codes[:, g, tokens].bitcast(FP8X4),
                    lhsT_scale=x_scales[:, g, tokens],
                    rhs=w_codes[:, g, :].bitcast(FP8X4),
                    rhs_scale=w_scales[:, g, :],
                    start=(g == 0),
                    stop=(g == PROJ_PASSES - 1),
                )
            sums_of[c, t] = sums

        def add_bias(c, t):
            if t == 0:
                v_new_of[c] = v_new_pool.tile([P, PACK, CHUNK_DIM], F32, name="v_new", tag="v_new")
            v_new = v_new_of[c]
            features = slice(c * CHUNK_DIM, (c + 1) * CHUNK_DIM)
            nc.vector.tensor_tensor(out=v_new[:, t, :], in0=sums_of[c, t][:], in1=bias_bf[:, features], op=ALU.add)
            nc.sync.dma_start(
                out=v_new_out[t // 2, t % 2, :, c * CHUNK_HEADS : (c + 1) * CHUNK_HEADS, :],
                in_=v_new[:, t, :].rearrange("p (h d) -> p h d", d=HEAD_DIM),
            )

        turned_q = {}
        turned_k = {}

        def turn_q(h):
            c, hh = divmod(h, CHUNK_HEADS)
            q_sb = heads_sb[c][0]
            q_turned = bank_psum.tile([P, NEW], BF16, tag="bank")
            for j in range(Q_TILES):
                nc.tensor.transpose(q_turned[:, j * P : (j + 1) * P], q_sb[:, hh * Q_TILES + j, :], ident_bf[:])
            q_t = head_pool.tile([P, NEW], BF16)
            nc.vector.tensor_copy(out=q_t[:], in_=q_turned[:])
            turned_q[h] = q_t

        def turn_k(h):
            c, hh = divmod(h, CHUNK_HEADS)
            k_turned = bank_psum.tile([P, KEYS], BF16, tag="bank")
            for part, k_sb in enumerate(heads_sb[c][1:3]):
                for j in range(Q_TILES):
                    first = part * CACHE + j * P
                    nc.tensor.transpose(k_turned[:, first : first + P], k_sb[:, hh * Q_TILES + j, :], ident_bf[:])
            k_t = head_pool.tile([P, KEYS], BF16)
            nc.scalar.copy(out=k_t[:], in_=k_turned[:])
            turned_k[h] = k_t

        row_sums_of = {}
        row_sum_of = {}
        inverse_of = {}
        v_grouped_of = {}
        v_mx = {}
        ctx_sums_of = {}

        def group_values(h, a, part):
            c, hh = divmod(h, CHUNK_HEADS)
            if a == 0:
                source = cached_sb[c][:, hh]
            else:
                source = v_new_of[c][:, :, hh * HEAD_DIM : (hh + 1) * HEAD_DIM]
            if part == 0:
                v_grouped_of[h, a] = v_pool.tile([P, HEAD_DIM, PACK], BF16, name="v_grouped_%d" % a, align_bytes=64)
            columns = slice(part * HEAD_DIM // V_PARTS, (part + 1) * HEAD_DIM // V_PARTS)
            nc.gpsimd.tensor_scalar(
                out=v_grouped_of[h, a][:, columns],
                in0=source[:, :, columns].rearrange("p t d -> p d t"),
                scalar1=1.0,
                scalar2=0.0,
                op0=ALU.mult,
                op1=ALU.add,
            )

        def add_row_sums(h):
            row_sum = head4_pool.tile([P, Q_TILES], F32)
            nc.gpsimd.tensor_tensor(
                out=row_sum[:], in0=row_sums_of[h][:, :, 0], in1=row_sums_of[h][:, :, 1], op=ALU.add
            )
            row_sum_of[h] = row_sum

        def quantise_values(h, a):
            if a == 0:
                v_codes = v_mx_pool.tile([P, 2 * HEAD_DIM], U32, align_bytes=64)
                v_scales = v_mx_pool.tile([P, 2 * HEAD_DIM], U8, align_bytes=64)
                v_mx[h] = (v_codes, v_scales)
            v_codes, v_scales = v_mx[h]
            columns = slice(a * HEAD_DIM, (a + 1) * HEAD_DIM)
            nc.vector.quantize_mx(
                out=v_codes[:, columns].bitcast(FP8X4),
                scales=v_scales[:, columns],
                in_=v_grouped_of[h, a][:].rearrange("p d t -> p (d t)"),
            )

        def invert_row_sums(h):
            inverse = head4_pool.tile([P, Q_TILES], F32)
            nc.vector.reciprocal(out=inverse[:], in_=row_sum_of[h][:])
            inverse_of[h] = inverse

        def multiply_e_v(h, units):
            v_codes, v_scales = v_mx[h]
            ctx_sums = bank_psum.tile([P, Q_TILES * HEAD_DIM], F32, tag="bank")
            for n in units:
                i = unit(n)[1]
                e_codes, e_scales = e_mx[n]
                for a in range(2):
                    columns = slice(a * P, (a + 1) * P)
                    nc.tensor.matmul_mx(
                        out=ctx_sums[:, i * HEAD_DIM : (i + 1) * HEAD_DIM],
                        lhsT=e_codes[:, columns].bitcast(FP8X4),
                        lhsT_scale=e_scales[:, columns],
                        rhs=v_codes[:, columns].bitcast(FP8X4),
                        rhs_scale=v_scales[:, columns],
                        start=(a == 0),
                        stop=(a == 1),
                    )
                ctx_sums_of[h, i] = ctx_sums

        def divide_and_store(h, first, count):
            tiles = slice(first, first + count)
            ctx = ctx_pool.tile([P, Q_TILES, HEAD_DIM], F32)
            nc.vector.tensor_tensor(
                out=ctx[:, tiles, :],
                in0=ctx_sums_of[h, first][:].rearrange("p (i d) -> p i d", d=HEAD_DIM)[:, tiles, :],
                in1=inverse_of[h][:, tiles].unsqueeze(2).to_broadcast([P, count, HEAD_DIM]),
                op=ALU.mult,
            )
            nc.sync.dma_start(
                out=ctx_out[first * P : (first + count) * P, h * HEAD_DIM : (h + 1) * HEAD_DIM].rearrange(
                    "(i p) d -> p i d", p=P
                ),
                in_=ctx[:, tiles, :],
            )

        scores_of = {}
        maxima_of = {}
        shift_of = {}
        e_grouped_of = {}
        e_mx = {}

        def scores(n):
            h, i = unit(n)
            q_t, k_t = turned_q[h], turned_k[h]
            queries = slice(i * P, (i + 1) * P)
            before = i * P
            seen_new = before + P
            keeps_clock = n not in head_of_round and n not in project_of_round
            s_cache = bank_psum.tile([P, CACHE], F32, tag="bank")
            if keeps_clock:
                nc.tensor.matmul(out=s_cache[:, 0:P], lhsT=q_t[:, queries], rhs=k_t[:, 0:P], start=True, stop=True)
            nc.tensor.matmul(out=s_cache[:], lhsT=q_t[:, queries], rhs=k_t[:, 0:CACHE], start=True, stop=True)
            s_new = bank_psum.tile([P, NEW], F32, tag="bank")
            width = NEW if keeps_clock else seen_new
            nc.tensor.matmul(
                out=s_new[:, 0:width],
                lhsT=q_t[:, queries],
                rhs=k_t[:, CACHE : CACHE + width],
                start=True,
                stop=False,
            )
            nc.tensor.matmul(out=s_new[:, before:seen_new], lhsT=ident_bf[:], rhs=mask_bf[:], start=False, stop=True)
            scores_of[n] = (s_cache, s_new)

        def find_maxima(n):
            h, i = unit(n)
            seen_new = (i + 1) * P
            s_cache, s_new = scores_of[n]
            maxima = unit_pool.tile([P, 2], F32)
            nc.vector.tensor_reduce(out=maxima[:, 0:1], in_=s_cache[:], axis=AXIS_X, op=ALU.max)
            nc.vector.tensor_reduce(out=maxima[:, 1:2], in_=s_new[:, 0:seen_new], axis=AXIS_X, op=ALU.max)
            maxima_of[n] = maxima

        def shift(n):
            maxima = maxima_of[n]
            minus_max = unit_pool.tile([P, 1], F32)
            nc.vector.tensor_scalar(
                out=minus_max[:],
                in0=maxima[:, 0:1],
                scalar1=maxima[:, 1:2],
                scalar2=-SCORE_SCALE,
                op0=ALU.max,
                op1=ALU.mult,
            )
            shift_of[n] = minus_max

        def exponentials(n):
            h, i = unit(n)
            if n % Q_TILES == 0:
                row_sums_of[h] = head4_pool.tile([P, Q_TILES, 2], F32, name="row_sums")
            s_cache, s_new = scores_of[n]
            seen_new = (i + 1) * P
            e_sb = e_rows[i, h % 2]
            nc.scalar.activation(
                out=e_sb[:, 0:CACHE],
                in_=s_cache[:],
                func=ACT.Exp,
                bias=shift_of[n][:],
                scale=SCORE_SCALE,
                accum_out=row_sums_of[h][:, i, 0:1],
            )
            nc.scalar.activation(
                out=e_sb[:, CACHE : CACHE + seen_new],
                in_=s_new[:, 0:seen_new],
                func=ACT.Exp,
                bias=shift_of[n][:],
                scale=SCORE_SCALE,
                accum_out=row_sums_of[h][:, i, 1:2],
            )

        def turn_e(n):
            h, i = unit(n)
            e_words = e_rows[i, h % 2][:].bitcast(F32)
            e_turned = bank_psum.tile([P, 512], F32, tag="bank")
            for j in range(KEYS // (2 * P)):
                nc.tensor.transpose(e_turned[:, j * P : (j + 1) * P], e_words[:, j * P : (j + 1) * P], ident_f32[:])
            e_grouped = unit_pool.tile([P, 2 * P * PACK], BF16, align_bytes=64)
            nc.scalar.copy(
                out=e_grouped[:].bitcast(F32).rearrange("p (a m u) -> p a m u", a=2, u=2),
                in_=e_turned[:].rearrange("p (a u m) -> p a m u", a=2, u=2),
            )
            e_grouped_of[n] = e_grouped

        def quantise_e(n):
            e_codes = e_mx_pool.tile([P, 2 * P], U32, align_bytes=64)
            e_scales = e_mx_pool.tile([P, 2 * P], U8, align_bytes=64)
            nc.vector.quantize_mx(out=e_codes[:].bitcast(FP8X4), scales=e_scales[:], in_=e_grouped_of[n][:])
            e_mx[n] = (e_codes, e_scales)

        pieces_of_round = piece_rounds()
        project_of_round = {}
        ready = {}
        for c in range(CHUNKS):
            first = max(FIRST_PROJECT_ROUND + c * PACK * MX_STEP, last_round(pieces_of_round, c) + 1)
            for t in range(PACK):
                project_of_round[first + MX_STEP * t] = (c, t)
            ready[c] = first + MX_STEP * (PACK - 1) + 1
        pv_rounds = []
        for h in range(HEADS):
            earliest = max(Q_TILES * h + PV_LAG, ready[h // CHUNK_HEADS] + GROUP_V_LEAD + 1)
            pv_rounds.append(max(earliest, pv_rounds[-1] + MX_STEP) if h else earliest)
        last_head = HEADS - 1
        last_units = range(UNITS - Q_TILES, UNITS)
        head_of_round = {number: h for h, number in enumerate(pv_rounds[:last_head])}
        pv_rounds[last_head] = last_units[0] + QUANTISE_LAG
        quantise_of_round = {number - QUANTISE_V_LEAD: h for h, number in enumerate(pv_rounds)}
        sum_of_round = {number - ROW_SUM_LEAD: h for number, h in head_of_round.items()}
        sum_of_round[UNITS + EXP_LAG] = last_head

        def reload_weights(c):
            weights_sb[c] = new_weights()
            for half in range(2):
                load_weights(c, weights_sb[c], half)

        cached_rounds = [max(Q_TILES * h + CACHED_LAG, FIRST_CACHED_ROUND + CACHED_STEP * h) for h in range(HEADS)]
        groups_of_round = {}
        for h in range(HEADS):
            for part in range(V_PARTS):
                groups_of_round.setdefault(cached_rounds[h] - V_PARTS + part, []).append((h, 0, part))
                groups_of_round.setdefault(pv_rounds[h] - GROUP_V_LEAD + part, []).append((h, 1, part))

        def spread_bias(c, copy):
            features = slice(c * CHUNK_DIM, (c + 1) * CHUNK_DIM)
            spread = bank_psum.tile([P, CHUNK_DIM], F32, name="spread", tag="bank")
            nc.tensor.matmul(out=spread[:], lhsT=ones[:], rhs=bias_rows[:, features], start=True, stop=True)
            copy(out=bias_bf[:, features], in_=spread[:])

        unread = bank_psum.tile([P, CACHE], F32, name="unread", tag="bank")
        for i in range(4):
            nc.tensor.matmul(out=unread[:], lhsT=zeros[:, 0:P], rhs=zeros[:], start=True, stop=True)
        turn_q(0)
        turn_k(0)
        for c in range(CHUNKS):
            spread_bias(c, nc.vector.tensor_copy if c % 2 == 0 else nc.scalar.copy)
        waiting = []
        for n in range(ROUNDS):
            if n < UNITS:
                scores(n)
            between = bool(waiting) or n in quantise_of_round or n in cached_rounds
            if between and 0 <= n - QUANTISE_LAG < UNITS:
                quantise_e(n - QUANTISE_LAG)
            if n - 1 in head_of_round:
                divide_and_store(head_of_round[n - 1], 0, Q_TILES)
            if n - QUANTISE_LAG - LAST_DIVIDE_LAG in last_units:
                divide_and_store(last_head, unit(n - QUANTISE_LAG - LAST_DIVIDE_LAG)[1], 1)
            if n - 1 in project_of_round:
                add_bias(*project_of_round[n - 1])
            for h, a, part in groups_of_round.get(n, []):
                group_values(h, a, part)
                c, last = divmod(h, CHUNK_HEADS)
                if (last, a, part) == (CHUNK_HEADS - 1, 0, V_PARTS - 1) and c + 2 < CHUNKS:
                    cached_sb[c + 2] = load_cached_values(c + 2)
            if n in sum_of_round:
                add_row_sums(sum_of_round[n])
            if n < UNITS:
                find_maxima(n)
            if not between and 0 <= n - QUANTISE_LAG < UNITS:
                quantise_e(n - QUANTISE_LAG)
            if n in quantise_of_round:
                quantise_values(quantise_of_round[n], 1)
            if n - 1 in sum_of_round:
                invert_row_sums(sum_of_round[n - 1])
            for h in range(HEADS):
                if n == cached_rounds[h]:
                    quantise_values(h, 0)
            for piece in waiting:
                quantise_rows(*piece)
            waiting = []
            if n < UNITS:
                shift(n)
            if 0 <= n - EXP_LAG < UNITS:
                exponentials(n - EXP_LAG)
            if 0 <= n - TURN_LAG < UNITS - 2:
                turn_e(n - TURN_LAG)
            if n - LAST_TURN_LAG in (UNITS - 2, UNITS - 1):
                turn_e(n - LAST_TURN_LAG)

            h, late = divmod(n + Q_LEAD, Q_TILES)
            if late == 0 and 0 < h < HEADS:
                turn_q(h)
            h, late = divmod(n + K_LEAD, Q_TILES)
            if late == 0 and 0 < h < HEADS:
                turn_k(h)
                c, last = divmod(h, CHUNK_HEADS)
                if last == CHUNK_HEADS - 1 and c + 2 < CHUNKS:
                    heads_sb[c + 2] = new_heads()
                    load_heads(c + 2, heads_sb[c + 2], 0, CHUNK_HEADS)
            for source, half, g in pieces_of_round.get(n, []):
                if source == "x":
                    rows_sb, target = x_sb, (x_codes, x_scales)
                else:
                    if (half, g) == (0, 0):
                        weights_mx[source] = new_weights_mx()
                    rows_sb, target = weights_sb[source], weights_mx[source]
                by_vector = source in ("x", 0) and g % 2 == 0
                copy = nc.vector.tensor_copy if by_vector else nc.scalar.copy
                waiting.append((turn_rows(rows_sb, half, g, copy), half, g) + target)
                if (half, g) == (1, PROJ_PASSES - 1) and source == "x":
                    reload_weights(2)
                if (half, g) == (1, PROJ_PASSES - 1) and source == 0:
                    reload_weights(3)

            if n in head_of_round:
                h = head_of_round[n]
                multiply_e_v(h, range(h * Q_TILES, (h + 1) * Q_TILES))
            if n - QUANTISE_LAG in last_units:
                multiply_e_v(last_head, [n - QUANTISE_LAG])
            if n in project_of_round:
                project(*project_of_round[n])
